import numpy as np
import ml_dtypes


def mxq(x, axis, fmt="e4m3"):
    dtype, down = {"e4m3": (ml_dtypes.float8_e4m3fn, 7), "e5m2": (ml_dtypes.float8_e5m2, 14)}[fmt]
    v = np.moveaxis(np.asarray(x, np.float32).astype(ml_dtypes.bfloat16).astype(np.float64), axis, -1)
    blocks = v.reshape(v.shape[:-1] + (-1, 32))
    amax = np.abs(blocks).max(-1, keepdims=True)
    byte = np.maximum(np.where(amax > 0, np.frexp(amax)[1] - 1 + 127, 0) - down, 1)
    scale = np.exp2(byte - 127.0)
    codes = (blocks / scale).astype(np.float32).astype(dtype).astype(np.float64)
    return np.moveaxis((codes * scale).reshape(v.shape), -1, axis)


WIDE = False


def mx_kscale(k):
    if not WIDE:
        return np.ones(k)
    levels = np.array([10, -10, 5, -5, 0])
    a = np.random.permutation(np.resize(levels, k // 512 * 4)).reshape(k // 512, 4)
    idx = np.arange(k)
    return np.exp2(a[idx // 512, idx % 128 // 32])


BF16 = ml_dtypes.bfloat16


def bf(x):
    return np.asarray(x, np.float32).astype(BF16)


def f64(x):
    return np.asarray(x).astype(np.float64)


BS, N, Bb, Cc, D, H, DP = 2, 64, 1, 1, 512, 1024, 512
G = Bb * Cc
P = 4 * D


def gmm(x, w):
    return (mxq(x, 3, "e4m3").transpose(0, 2, 1, 3) @ mxq(w, 1, "e4m3")).transpose(0, 2, 1, 3)


def unit_normalize(x):
    return x / np.maximum(np.sqrt((x * x).sum(-1, keepdims=True)), 1e-6)


def setup_inputs():
    s = mx_kscale(H)
    rn = np.random.standard_normal
    a = rn((BS, N, G, H))
    return {
        "ffn_act": bf(a / (1.0 + np.exp(-1.702 * a)) * s),
        "x_mix": bf(rn((BS, N, G, D))),
        "down_w": bf(rn((G, H, D)) / np.sqrt(H) / s[:, None]),
        "down_b": bf(0.1 * rn((G, D))),
        "post_w": bf(rn((G, D, P)) / np.sqrt(D)),
        "post_b": bf(0.1 * rn((G, P))),
    }


def reference(ffn_act, x_mix, down_w, down_b, post_w, post_b):
    x_out = f64(x_mix) + (gmm(f64(ffn_act), f64(down_w)) + f64(down_b))
    proj = (gmm(x_out, f64(post_w)) + f64(post_b)).reshape(BS, N, Bb, Cc, P)
    k_pre, v_post, k_cand_raw, v_cand = np.split(proj, 4, axis=-1)
    k_cand = unit_normalize(k_pre)
    q_nov = unit_normalize(k_cand_raw)
    return x_out, k_cand, v_post, q_nov, v_cand

@@ -1,0 +1,189 @@
+import concourse.mybir as mybir
+from concourse.masks import make_identity
+
+F32 = mybir.dt.float32
+BF16 = mybir.dt.bfloat16
+I32 = mybir.dt.int32
+U32 = mybir.dt.uint32
+U8 = mybir.dt.uint8
+FP8X4 = mybir.dt.float8_e4m3fn_x4
+ACT = mybir.ActivationFunctionType
+ALU = mybir.AluOpType
+
+P = 128
+PACK = 4
+K_PASS = P * PACK
+H = 1024
+D = 512
+RUN = 512
+RUNS = 4
+H_PASSES = H // K_PASS
+BIAS_ROW = 2 * P
+DOWN_ROWS = D // BIAS_ROW
+BIAS_ROWS = (D + RUNS * RUN) // BIAS_ROW
+ROWS_PER_BANK = 4
+NORMALISED = (0, 2)
+PLAIN = (1, 3)
+RUN_ORDER = NORMALISED + PLAIN
+EPS = 1e-6
+
+FLOPS = 2 * P * (H * D + D * RUNS * RUN)
+
+
+def regroup(nc, grouped, raw):
+    width = raw.shape[2]
+    half = width // 2
+    for copy, cols in ((nc.vector.tensor_copy, slice(0, half)), (nc.scalar.copy, slice(half, width))):
+        copy(
+            out=grouped[:, cols, :].rearrange("p (c i) t -> p c t i", i=4),
+            in_=raw[:, :, cols].rearrange("p t (c i) -> p c t i", i=4),
+        )
+
+
+def quantise(nc, codes, scales, grouped):
+    nc.vector.quantize_mx(out=codes.bitcast(FP8X4), scales=scales, in_=grouped)
+
+
+def tile_corticalcolumngroup_pb_s_kernel(
+    tc, ffn_act, x_mix, down_w, down_b, post_w, post_b, out_0, out_1, out_2, out_3, out_4
+):
+    nc = tc.nc
+    run_out = (out_1, out_2, out_3, out_4)
+
+    with tc.tile_pool(name="keep", bufs=1) as keep, tc.psum_pool(name="psum", bufs=8) as psum:
+        ident = keep.tile([P, P], F32)
+        make_identity(nc, ident[:])
+        one = keep.tile([P, 1], F32)
+        nc.vector.memset(one[:], 1.0)
+        warm = keep.tile([P, 1], F32)
+        nc.scalar.activation(out=warm[:], in_=one[:], func=ACT.Sqrt)
+        bias_rows = keep.tile([P, BIAS_ROW], BF16)
+        nc.vector.memset(bias_rows[:].bitcast(I32), 0)
+
+        nc.sync.dma_start(
+            out=bias_rows[0:DOWN_ROWS, :], in_=down_b.rearrange("o (r c) -> (o r) c", c=BIAS_ROW)
+        )
+        nc.sync.dma_start(
+            out=bias_rows[DOWN_ROWS:BIAS_ROWS, :], in_=post_b.rearrange("o (r c) -> (o r) c", c=BIAS_ROW)
+        )
+        act_sb = keep.tile([P, H], BF16)
+        nc.sync.dma_start(out=act_sb[:], in_=ffn_act.rearrange("s n g h -> (s n g) h"))
+        down_rows = down_w.rearrange("o (g u p e) n -> (o g) p u (e n)", g=H_PASSES, u=2, e=2)
+        down_raw = []
+        for g in range(H_PASSES):
+            raw = keep.tile([P, PACK, D], BF16, name="down_raw%d" % g)
+            nc.sync.dma_start(out=raw[:].rearrange("p (u e) n -> p u (e n)", u=2), in_=down_rows[g])
+            down_raw.append(raw)
+        mix_sb = keep.tile([P, D], BF16)
+        nc.sync.dma_start(out=mix_sb[:], in_=x_mix.rearrange("s n g d -> (s n g) d"))
+        post_rows = post_w.rearrange("o (t p) n -> (o p) t n", t=PACK)
+        post_raw = {}
+        for r in RUN_ORDER:
+            raw = keep.tile([P, PACK, RUN], BF16, name="post_raw%d" % r)
+            nc.sync.dma_start(out=raw[:], in_=post_rows[:, :, r * RUN : (r + 1) * RUN])
+            post_raw[r] = raw
+
+        bias_col_ps = psum.tile([P, P], F32, tag="bank")
+        nc.tensor.transpose(bias_col_ps[:], bias_rows[:].bitcast(F32), ident[:])
+        bias_col = keep.tile([P, BIAS_ROWS], F32)
+        nc.vector.tensor_copy(out=bias_col[:], in_=bias_col_ps[:, 0:BIAS_ROWS])
+        bias_all = keep.tile([P, BIAS_ROWS * BIAS_ROW], BF16)
+        bias_words = bias_all[:].bitcast(F32)
+        for first in range(0, BIAS_ROWS, ROWS_PER_BANK):
+            rows = min(ROWS_PER_BANK, BIAS_ROWS - first)
+            bias_ps = psum.tile([P, rows * P], F32, tag="bank", name="bias_ps%d" % first)
+            for i in range(rows):
+                nc.tensor.transpose(
+                    bias_ps[:, i * P : (i + 1) * P],
+                    bias_col[:, first + i : first + i + 1].to_broadcast([P, P]),
+                    ident[:],
+                )
+            nc.vector.tensor_copy(out=bias_words[:, first * P : (first + rows) * P], in_=bias_ps[:])
+
+        act_words = act_sb[:].bitcast(F32)
+        act_ps = psum.tile([P, 2 * H_PASSES, P], F32, tag="bank")
+        for j in range(2 * H_PASSES):
+            nc.tensor.transpose(act_ps[:, j, :], act_words[:, j * P : (j + 1) * P], ident[:])
+        act_grouped = keep.tile([P, H_PASSES * P * PACK], BF16, align_bytes=64)
+        nc.scalar.copy(
+            out=act_grouped[:].bitcast(F32).rearrange("p (g r u) -> p g r u", g=H_PASSES, u=2),
+            in_=act_ps[:].rearrange("p (g u) r -> p g r u", u=2),
+        )
+        act_codes = keep.tile([P, H_PASSES * P], U32, align_bytes=64)
+        act_scales = keep.tile([P, H_PASSES * P], U8, align_bytes=64)
+        quantise(nc, act_codes[:], act_scales[:], act_grouped[:])
+
+        down_codes = keep.tile([P, H_PASSES, D], U32, align_bytes=64)
+        down_scales = keep.tile([P, H_PASSES, D], U8, align_bytes=64)
+        for g in range(H_PASSES):
+            grouped = keep.tile([P, D, PACK], BF16, align_bytes=64, name="down_grouped%d" % g)
+            regroup(nc, grouped, down_raw[g])
+            quantise(nc, down_codes[:, g, :], down_scales[:, g, :], grouped[:].rearrange("p n t -> p (n t)"))
+
+        mix_bias = keep.tile([P, D], F32)
+        nc.vector.tensor_tensor(out=mix_bias[:], in0=mix_sb[:], in1=bias_all[:, 0:D], op=ALU.add)
+        down_ps = psum.tile([P, D], F32, tag="bank")
+        for g in range(H_PASSES):
+            tokens = slice(g * P, (g + 1) * P)
+            nc.tensor.matmul_mx(
+                out=down_ps[:],
+                lhsT=act_codes[:, tokens].bitcast(FP8X4),
+                lhsT_scale=act_scales[:, tokens],
+                rhs=down_codes[:, g, :].bitcast(FP8X4),
+                rhs_scale=down_scales[:, g, :],
+                start=(g == 0),
+                stop=(g == H_PASSES - 1),
+            )
+        x_out = keep.tile([P, D], F32)
+        nc.vector.tensor_tensor(out=x_out[:], in0=down_ps[:], in1=mix_bias[:], op=ALU.add)
+        nc.sync.dma_start(out=out_0.rearrange("s n g d -> (s n g) d"), in_=x_out[:])
+
+        x_ps = psum.tile([P, PACK, P], F32, tag="bank")
+        for t in range(PACK):
+            nc.tensor.transpose(x_ps[:, t, :], x_out[:, t * P : (t + 1) * P], ident[:])
+        x_grouped = keep.tile([P, P, PACK], BF16, align_bytes=64)
+        nc.scalar.copy(out=x_grouped[:], in_=x_ps[:].rearrange("p t r -> p r t"))
+        x_codes = keep.tile([P, P], U32, align_bytes=64)
+        x_scales = keep.tile([P, P], U8, align_bytes=64)
+        quantise(nc, x_codes[:], x_scales[:], x_grouped[:].rearrange("p r t -> p (r t)"))
+
+        post_codes = keep.tile([P, RUNS, RUN], U32, align_bytes=64)
+        post_scales = keep.tile([P, RUNS, RUN], U8, align_bytes=64)
+        for r in RUN_ORDER:
+            grouped = keep.tile([P, RUN, PACK], BF16, align_bytes=64, name="post_grouped%d" % r)
+            regroup(nc, grouped, post_raw[r])
+            quantise(nc, post_codes[:, r, :], post_scales[:, r, :], grouped[:].rearrange("p n t -> p (n t)"))
+
+        proj = {}
+        for r in RUN_ORDER:
+            proj_ps = psum.tile([P, RUN], F32, tag="bank", name="proj_ps%d" % r)
+            nc.tensor.matmul_mx(
+                out=proj_ps[:],
+                lhsT=x_codes[:].bitcast(FP8X4),
+                lhsT_scale=x_scales[:],
+                rhs=post_codes[:, r, :].bitcast(FP8X4),
+                rhs_scale=post_scales[:, r, :],
+                start=True,
+                stop=True,
+            )
+            proj[r] = keep.tile([P, RUN], F32, name="proj%d" % r)
+            nc.vector.tensor_tensor(
+                out=proj[r][:], in0=proj_ps[:], in1=bias_all[:, D + r * RUN : D + (r + 1) * RUN], op=ALU.add
+            )
+            if r in PLAIN:
+                nc.sync.dma_start(out=run_out[r].flatten_outer_dims(), in_=proj[r][:])
+
+        sum_sq = keep.tile([P, len(NORMALISED)], F32)
+        for i, r in enumerate(NORMALISED):
+            squares = keep.tile([P, RUN], F32, name="squares%d" % r)
+            nc.scalar.activation(out=squares[:], in_=proj[r][:], func=ACT.Square, accum_out=sum_sq[:, i : i + 1])
+        floored = keep.tile([P, len(NORMALISED)], F32)
+        nc.vector.tensor_scalar_max(out=floored[:], in0=sum_sq[:], scalar1=EPS * EPS)
+        norm = keep.tile([P, len(NORMALISED)], F32)
+        nc.scalar.activation(out=norm[:], in_=floored[:], func=ACT.Sqrt)
+        inv_norm = keep.tile([P, len(NORMALISED)], F32)
+        nc.vector.reciprocal(out=inv_norm[:], in_=norm[:])
+        for i, r in enumerate(NORMALISED):
+            unit = keep.tile([P, RUN], F32, name="unit%d" % r)
+            nc.scalar.activation(out=unit[:], in_=proj[r][:], func=ACT.Copy, scale=inv_norm[:, i : i + 1])
+            nc.sync.dma_start(out=run_out[r].flatten_outer_dims(), in_=unit[:])

@@ -20,20 +20,22 @@ RUNS = 4
 H_PASSES = H // K_PASS
 BIAS_ROW = 2 * P
 DOWN_ROWS = D // BIAS_ROW
-BIAS_ROWS = (D + RUNS * RUN) // BIAS_ROW
-ROWS_PER_BANK = 4
+RUN_ROWS = RUN // BIAS_ROW
+BIAS_ROWS = DOWN_ROWS + RUNS * RUN_ROWS
+RUNS_PER_BANK = 2
 NORMALISED = (0, 2)
 PLAIN = (1, 3)
 RUN_ORDER = NORMALISED + PLAIN
 EPS = 1e-6
+DOWN_VECTOR_COLS = 320
+POST_VECTOR_COLS = 256
 
 FLOPS = 2 * P * (H * D + D * RUNS * RUN)
 
 
-def regroup(nc, grouped, raw):
+def regroup(nc, grouped, raw, vector_cols):
     width = raw.shape[2]
-    half = width // 2
-    for copy, cols in ((nc.vector.tensor_copy, slice(0, half)), (nc.scalar.copy, slice(half, width))):
+    for copy, cols in ((nc.vector.tensor_copy, slice(0, vector_cols)), (nc.scalar.copy, slice(vector_cols, width))):
         copy(
             out=grouped[:, cols, :].rearrange("p (c i) t -> p c t i", i=4),
             in_=raw[:, :, cols].rearrange("p t (c i) -> p c t i", i=4),
@@ -50,112 +52,71 @@ def tile_corticalcolumngroup_pb_s_kernel(
     nc = tc.nc
     run_out = (out_1, out_2, out_3, out_4)
 
-    with tc.tile_pool(name="keep", bufs=1) as keep, tc.psum_pool(name="psum", bufs=8) as psum:
-        ident = keep.tile([P, P], F32)
-        make_identity(nc, ident[:])
-        one = keep.tile([P, 1], F32)
-        nc.vector.memset(one[:], 1.0)
-        warm = keep.tile([P, 1], F32)
-        nc.scalar.activation(out=warm[:], in_=one[:], func=ACT.Sqrt)
+    with tc.tile_pool(name="keep", bufs=1) as keep, tc.psum_pool(name="psum", bufs=8) as psum, tc.manual_schedule():
+
+        act_sb = keep.tile([P, H], BF16)
+        nc.sync.dma_start(out=act_sb[:], in_=ffn_act.rearrange("s n g h -> (s n g) h"))
         bias_rows = keep.tile([P, BIAS_ROW], BF16)
         nc.vector.memset(bias_rows[:].bitcast(I32), 0)
-
         nc.sync.dma_start(
             out=bias_rows[0:DOWN_ROWS, :], in_=down_b.rearrange("o (r c) -> (o r) c", c=BIAS_ROW)
         )
         nc.sync.dma_start(
             out=bias_rows[DOWN_ROWS:BIAS_ROWS, :], in_=post_b.rearrange("o (r c) -> (o r) c", c=BIAS_ROW)
         )
-        act_sb = keep.tile([P, H], BF16)
-        nc.sync.dma_start(out=act_sb[:], in_=ffn_act.rearrange("s n g h -> (s n g) h"))
         down_rows = down_w.rearrange("o (g u p e) n -> (o g) p u (e n)", g=H_PASSES, u=2, e=2)
         down_raw = []
         for g in range(H_PASSES):
-            raw = keep.tile([P, PACK, D], BF16, name="down_raw%d" % g)
-            nc.sync.dma_start(out=raw[:].rearrange("p (u e) n -> p u (e n)", u=2), in_=down_rows[g])
-            down_raw.append(raw)
+            down_raw.append(keep.tile([P, PACK, D], BF16, name="down_raw%d" % g))
+            nc.sync.dma_start(out=down_raw[g][:].rearrange("p (u e) n -> p u (e n)", u=2), in_=down_rows[g])
         mix_sb = keep.tile([P, D], BF16)
         nc.sync.dma_start(out=mix_sb[:], in_=x_mix.rearrange("s n g d -> (s n g) d"))
         post_rows = post_w.rearrange("o (t p) n -> (o p) t n", t=PACK)
         post_raw = {}
         for r in RUN_ORDER:
-            raw = keep.tile([P, PACK, RUN], BF16, name="post_raw%d" % r)
-            nc.sync.dma_start(out=raw[:], in_=post_rows[:, :, r * RUN : (r + 1) * RUN])
-            post_raw[r] = raw
+            post_raw[r] = keep.tile([P, PACK, RUN], BF16, name="post_raw%d" % r)
+            nc.sync.dma_start(out=post_raw[r][:], in_=post_rows[:, :, r * RUN : (r + 1) * RUN])
 
-        bias_col_ps = psum.tile([P, P], F32, tag="bank")
-        nc.tensor.transpose(bias_col_ps[:], bias_rows[:].bitcast(F32), ident[:])
-        bias_col = keep.tile([P, BIAS_ROWS], F32)
-        nc.vector.tensor_copy(out=bias_col[:], in_=bias_col_ps[:, 0:BIAS_ROWS])
-        bias_all = keep.tile([P, BIAS_ROWS * BIAS_ROW], BF16)
-        bias_words = bias_all[:].bitcast(F32)
-        for first in range(0, BIAS_ROWS, ROWS_PER_BANK):
-            rows = min(ROWS_PER_BANK, BIAS_ROWS - first)
-            bias_ps = psum.tile([P, rows * P], F32, tag="bank", name="bias_ps%d" % first)
+        ident = keep.tile([P, P], F32)
+        make_identity(nc, ident[:])
+        one = keep.tile([P, 1], F32)
+        nc.vector.memset(one[:], 1.0)
+        warm = keep.tile([P, 1], F32)
+        nc.scalar.activation(out=warm[:], in_=one[:], func=ACT.Abs_reciprocal_sqrt)
+
+        post_bias = keep.tile([P, RUNS * RUN], BF16)
+        down_grouped = [keep.tile([P, D, PACK], BF16, align_bytes=64, name="down_grouped%d" % g) for g in range(H_PASSES)]
+        down_codes = keep.tile([P, H_PASSES, D], U32, align_bytes=64)
+        down_scales = keep.tile([P, H_PASSES, D], U8, align_bytes=64)
+        post_grouped = {}
+        for r in RUN_ORDER:
+            post_grouped[r] = keep.tile([P, RUN, PACK], BF16, align_bytes=64, name="post_grouped%d" % r)
+        post_codes = keep.tile([P, RUNS, RUN], U32, align_bytes=64)
+        post_scales = keep.tile([P, RUNS, RUN], U8, align_bytes=64)
+        x_codes = keep.tile([P, P], U32, align_bytes=64)
+        x_scales = keep.tile([P, P], U8, align_bytes=64)
+        proj = {}
+
+        def spread_bias_rows(first, rows):
+            bank = psum.tile([P, rows * P], F32, tag="bank", name="bias_ps%d" % first)
             for i in range(rows):
                 nc.tensor.transpose(
-                    bias_ps[:, i * P : (i + 1) * P],
+                    bank[:, i * P : (i + 1) * P],
                     bias_col[:, first + i : first + i + 1].to_broadcast([P, P]),
                     ident[:],
                 )
-            nc.vector.tensor_copy(out=bias_words[:, first * P : (first + rows) * P], in_=bias_ps[:])
+            return bank
 
-        act_words = act_sb[:].bitcast(F32)
-        act_ps = psum.tile([P, 2 * H_PASSES, P], F32, tag="bank")
-        for j in range(2 * H_PASSES):
-            nc.tensor.transpose(act_ps[:, j, :], act_words[:, j * P : (j + 1) * P], ident[:])
-        act_grouped = keep.tile([P, H_PASSES * P * PACK], BF16, align_bytes=64)
-        nc.scalar.copy(
-            out=act_grouped[:].bitcast(F32).rearrange("p (g r u) -> p g r u", g=H_PASSES, u=2),
-            in_=act_ps[:].rearrange("p (g u) r -> p g r u", u=2),
-        )
-        act_codes = keep.tile([P, H_PASSES * P], U32, align_bytes=64)
-        act_scales = keep.tile([P, H_PASSES * P], U8, align_bytes=64)
-        quantise(nc, act_codes[:], act_scales[:], act_grouped[:])
+        def regroup_post(r):
+            regroup(nc, post_grouped[r], post_raw[r], POST_VECTOR_COLS)
 
-        down_codes = keep.tile([P, H_PASSES, D], U32, align_bytes=64)
-        down_scales = keep.tile([P, H_PASSES, D], U8, align_bytes=64)
-        for g in range(H_PASSES):
-            grouped = keep.tile([P, D, PACK], BF16, align_bytes=64, name="down_grouped%d" % g)
-            regroup(nc, grouped, down_raw[g])
-            quantise(nc, down_codes[:, g, :], down_scales[:, g, :], grouped[:].rearrange("p n t -> p (n t)"))
+        def quantise_down(g):
+            quantise(nc, down_codes[:, g, :], down_scales[:, g, :], down_grouped[g][:].rearrange("p n t -> p (n t)"))
 
-        mix_bias = keep.tile([P, D], F32)
-        nc.vector.tensor_tensor(out=mix_bias[:], in0=mix_sb[:], in1=bias_all[:, 0:D], op=ALU.add)
-        down_ps = psum.tile([P, D], F32, tag="bank")
-        for g in range(H_PASSES):
-            tokens = slice(g * P, (g + 1) * P)
-            nc.tensor.matmul_mx(
-                out=down_ps[:],
-                lhsT=act_codes[:, tokens].bitcast(FP8X4),
-                lhsT_scale=act_scales[:, tokens],
-                rhs=down_codes[:, g, :].bitcast(FP8X4),
-                rhs_scale=down_scales[:, g, :],
-                start=(g == 0),
-                stop=(g == H_PASSES - 1),
-            )
-        x_out = keep.tile([P, D], F32)
-        nc.vector.tensor_tensor(out=x_out[:], in0=down_ps[:], in1=mix_bias[:], op=ALU.add)
-        nc.sync.dma_start(out=out_0.rearrange("s n g d -> (s n g) d"), in_=x_out[:])
+        def quantise_post(r):
+            quantise(nc, post_codes[:, r, :], post_scales[:, r, :], post_grouped[r][:].rearrange("p n t -> p (n t)"))
 
-        x_ps = psum.tile([P, PACK, P], F32, tag="bank")
-        for t in range(PACK):
-            nc.tensor.transpose(x_ps[:, t, :], x_out[:, t * P : (t + 1) * P], ident[:])
-        x_grouped = keep.tile([P, P, PACK], BF16, align_bytes=64)
-        nc.scalar.copy(out=x_grouped[:], in_=x_ps[:].rearrange("p t r -> p r t"))
-        x_codes = keep.tile([P, P], U32, align_bytes=64)
-        x_scales = keep.tile([P, P], U8, align_bytes=64)
-        quantise(nc, x_codes[:], x_scales[:], x_grouped[:].rearrange("p r t -> p (r t)"))
-
-        post_codes = keep.tile([P, RUNS, RUN], U32, align_bytes=64)
-        post_scales = keep.tile([P, RUNS, RUN], U8, align_bytes=64)
-        for r in RUN_ORDER:
-            grouped = keep.tile([P, RUN, PACK], BF16, align_bytes=64, name="post_grouped%d" % r)
-            regroup(nc, grouped, post_raw[r])
-            quantise(nc, post_codes[:, r, :], post_scales[:, r, :], grouped[:].rearrange("p n t -> p (n t)"))
-
-        proj = {}
-        for r in RUN_ORDER:
+        def project(r):
             proj_ps = psum.tile([P, RUN], F32, tag="bank", name="proj_ps%d" % r)
             nc.tensor.matmul_mx(
                 out=proj_ps[:],
@@ -168,22 +129,93 @@ def tile_corticalcolumngroup_pb_s_kernel(
             )
             proj[r] = keep.tile([P, RUN], F32, name="proj%d" % r)
             nc.vector.tensor_tensor(
-                out=proj[r][:], in0=proj_ps[:], in1=bias_all[:, D + r * RUN : D + (r + 1) * RUN], op=ALU.add
+                out=proj[r][:], in0=proj_ps[:], in1=post_bias[:, r * RUN : (r + 1) * RUN], op=ALU.add
             )
-            if r in PLAIN:
-                nc.sync.dma_start(out=run_out[r].flatten_outer_dims(), in_=proj[r][:])
 
-        sum_sq = keep.tile([P, len(NORMALISED)], F32)
-        for i, r in enumerate(NORMALISED):
+        def store_plain(r):
+            nc.sync.dma_start(out=run_out[r].flatten_outer_dims(), in_=proj[r][:])
+
+        def store_unit(r):
             squares = keep.tile([P, RUN], F32, name="squares%d" % r)
-            nc.scalar.activation(out=squares[:], in_=proj[r][:], func=ACT.Square, accum_out=sum_sq[:, i : i + 1])
-        floored = keep.tile([P, len(NORMALISED)], F32)
-        nc.vector.tensor_scalar_max(out=floored[:], in0=sum_sq[:], scalar1=EPS * EPS)
-        norm = keep.tile([P, len(NORMALISED)], F32)
-        nc.scalar.activation(out=norm[:], in_=floored[:], func=ACT.Sqrt)
-        inv_norm = keep.tile([P, len(NORMALISED)], F32)
-        nc.vector.reciprocal(out=inv_norm[:], in_=norm[:])
-        for i, r in enumerate(NORMALISED):
+            sum_sq = keep.tile([P, 1], F32, name="sum_sq%d" % r)
+            nc.scalar.activation(out=squares[:], in_=proj[r][:], func=ACT.Square, accum_out=sum_sq[:])
+            above = keep.tile([P, 1], F32, name="above%d" % r)
+            nc.scalar.activation(out=above[:], in_=sum_sq[:], func=ACT.Relu, bias=-EPS * EPS)
+            inv_norm = keep.tile([P, 1], F32, name="inv_norm%d" % r)
+            nc.scalar.activation(out=inv_norm[:], in_=above[:], func=ACT.Abs_reciprocal_sqrt, bias=EPS * EPS)
             unit = keep.tile([P, RUN], F32, name="unit%d" % r)
-            nc.scalar.activation(out=unit[:], in_=proj[r][:], func=ACT.Copy, scale=inv_norm[:, i : i + 1])
+            nc.scalar.activation(out=unit[:], in_=proj[r][:], func=ACT.Copy, scale=inv_norm[:])
             nc.sync.dma_start(out=run_out[r].flatten_outer_dims(), in_=unit[:])
+
+        act_words = act_sb[:].bitcast(F32)
+        act_ps = psum.tile([P, 2 * H_PASSES, P], F32, tag="bank")
+        for j in range(2 * H_PASSES):
+            nc.tensor.transpose(act_ps[:, j, :], act_words[:, j * P : (j + 1) * P], ident[:])
+        bias_col_ps = psum.tile([P, P], F32, tag="bank")
+        nc.tensor.transpose(bias_col_ps[:], bias_rows[:].bitcast(F32), ident[:])
+        bias_col = keep.tile([P, BIAS_ROWS], F32)
+        nc.vector.tensor_copy(out=bias_col[:], in_=bias_col_ps[:, 0:BIAS_ROWS])
+        down_bias_ps = spread_bias_rows(0, DOWN_ROWS)
+        post_bias_ps = [
+            spread_bias_rows(DOWN_ROWS + b * RUNS_PER_BANK * RUN_ROWS, RUNS_PER_BANK * RUN_ROWS)
+            for b in range(RUNS // RUNS_PER_BANK)
+        ]
+
+        act_grouped = keep.tile([P, H_PASSES * P * PACK], BF16, align_bytes=64)
+        nc.scalar.copy(
+            out=act_grouped[:].bitcast(F32).rearrange("p (g r u) -> p g r u", g=H_PASSES, u=2),
+            in_=act_ps[:].rearrange("p (g u) r -> p g r u", u=2),
+        )
+        regroup(nc, down_grouped[0], down_raw[0], DOWN_VECTOR_COLS)
+        act_codes = keep.tile([P, H_PASSES * P], U32, align_bytes=64)
+        act_scales = keep.tile([P, H_PASSES * P], U8, align_bytes=64)
+        quantise(nc, act_codes[:], act_scales[:], act_grouped[:])
+        regroup(nc, down_grouped[1], down_raw[1], DOWN_VECTOR_COLS)
+        quantise_down(0)
+        quantise_down(1)
+        down_ps = psum.tile([P, D], F32, tag="bank")
+        for g in range(H_PASSES):
+            tokens = slice(g * P, (g + 1) * P)
+            nc.tensor.matmul_mx(
+                out=down_ps[:],
+                lhsT=act_codes[:, tokens].bitcast(FP8X4),
+                lhsT_scale=act_scales[:, tokens],
+                rhs=down_codes[:, g, :].bitcast(FP8X4),
+                rhs_scale=down_scales[:, g, :],
+                start=(g == 0),
+                stop=(g == H_PASSES - 1),
+            )
+
+        bank_words = RUNS_PER_BANK * RUN // 2
+        for b in range(RUNS // RUNS_PER_BANK):
+            nc.scalar.copy(
+                out=post_bias[:].bitcast(F32)[:, b * bank_words : (b + 1) * bank_words], in_=post_bias_ps[b][:]
+            )
+        regroup_post(RUN_ORDER[0])
+        mix_bias = keep.tile([P, D], F32)
+        nc.vector.tensor_tensor(out=mix_bias[:], in0=down_bias_ps[:].bitcast(BF16), in1=mix_sb[:], op=ALU.add)
+        regroup_post(RUN_ORDER[1])
+        x_out = keep.tile([P, D], F32)
+        nc.vector.tensor_tensor(out=x_out[:], in0=down_ps[:], in1=mix_bias[:], op=ALU.add)
+        nc.sync.dma_start(out=out_0.rearrange("s n g d -> (s n g) d"), in_=x_out[:])
+        x_ps = psum.tile([P, PACK, P], F32, tag="bank")
+        for t in range(PACK):
+            nc.tensor.transpose(x_ps[:, t, :], x_out[:, t * P : (t + 1) * P], ident[:])
+        quantise_post(RUN_ORDER[0])
+        regroup_post(RUN_ORDER[2])
+        x_grouped = keep.tile([P, P, PACK], BF16, align_bytes=64)
+        nc.scalar.copy(out=x_grouped[:], in_=x_ps[:].rearrange("p t r -> p r t"))
+        quantise_post(RUN_ORDER[1])
+        quantise(nc, x_codes[:], x_scales[:], x_grouped[:].rearrange("p r t -> p (r t)"))
+        regroup_post(RUN_ORDER[3])
+
+        quantise_post(RUN_ORDER[2])
+        project(RUN_ORDER[0])
+        project(RUN_ORDER[1])
+        store_unit(RUN_ORDER[0])
+        quantise_post(RUN_ORDER[3])
+        project(RUN_ORDER[2])
+        store_plain(RUN_ORDER[2])
+        store_unit(RUN_ORDER[1])
+        project(RUN_ORDER[3])
+        store_plain(RUN_ORDER[3])

@@ -135,17 +135,19 @@ def tile_corticalcolumngroup_pb_s_kernel(
         def store_plain(r):
             nc.sync.dma_start(out=run_out[r].flatten_outer_dims(), in_=proj[r][:])
 
-        def store_unit(r):
-            squares = keep.tile([P, RUN], F32, name="squares%d" % r)
-            sum_sq = keep.tile([P, 1], F32, name="sum_sq%d" % r)
-            nc.scalar.activation(out=squares[:], in_=proj[r][:], func=ACT.Square, accum_out=sum_sq[:])
-            above = keep.tile([P, 1], F32, name="above%d" % r)
+        sum_sq = keep.tile([P, len(NORMALISED)], F32)
+        inv_norm = keep.tile([P, len(NORMALISED)], F32)
+
+        def sum_squares(i):
+            squares = keep.tile([P, RUN], F32, name="squares%d" % i)
+            nc.scalar.activation(
+                out=squares[:], in_=proj[NORMALISED[i]][:], func=ACT.Square, accum_out=sum_sq[:, i : i + 1]
+            )
+
+        def invert_norms():
+            above = keep.tile([P, len(NORMALISED)], F32)
             nc.scalar.activation(out=above[:], in_=sum_sq[:], func=ACT.Relu, bias=-EPS * EPS)
-            inv_norm = keep.tile([P, 1], F32, name="inv_norm%d" % r)
             nc.scalar.activation(out=inv_norm[:], in_=above[:], func=ACT.Abs_reciprocal_sqrt, bias=EPS * EPS)
-            unit = keep.tile([P, RUN], F32, name="unit%d" % r)
-            nc.scalar.activation(out=unit[:], in_=proj[r][:], func=ACT.Copy, scale=inv_norm[:])
-            nc.sync.dma_start(out=run_out[r].flatten_outer_dims(), in_=unit[:])
 
         act_words = act_sb[:].bitcast(F32)
         act_ps = psum.tile([P, 2 * H_PASSES, P], F32, tag="bank")
@@ -206,16 +208,20 @@ def tile_corticalcolumngroup_pb_s_kernel(
         x_grouped = keep.tile([P, P, PACK], BF16, align_bytes=64)
         nc.scalar.copy(out=x_grouped[:], in_=x_ps[:].rearrange("p t r -> p r t"))
         quantise_post(RUN_ORDER[1])
-        quantise(nc, x_codes[:], x_scales[:], x_grouped[:].rearrange("p r t -> p (r t)"))
         regroup_post(RUN_ORDER[3])
-
+        quantise(nc, x_codes[:], x_scales[:], x_grouped[:].rearrange("p r t -> p (r t)"))
         quantise_post(RUN_ORDER[2])
-        project(RUN_ORDER[0])
-        project(RUN_ORDER[1])
-        store_unit(RUN_ORDER[0])
         quantise_post(RUN_ORDER[3])
-        project(RUN_ORDER[2])
-        store_plain(RUN_ORDER[2])
-        store_unit(RUN_ORDER[1])
-        project(RUN_ORDER[3])
-        store_plain(RUN_ORDER[3])
+
+        for i in range(len(NORMALISED)):
+            project(NORMALISED[i])
+            sum_squares(i)
+        invert_norms()
+        for r in PLAIN:
+            project(r)
+            store_plain(r)
+        units = [keep.tile([P, RUN], F32, name="unit%d" % i) for i in range(len(NORMALISED))]
+        nc.vector.tensor_scalar_mul(out=units[0][:], in0=proj[NORMALISED[0]][:], scalar1=inv_norm[:, 0:1])
+        nc.scalar.activation(out=units[1][:], in_=proj[NORMALISED[1]][:], func=ACT.Copy, scale=inv_norm[:, 1:2])
+        for i, r in enumerate(NORMALISED):
+            nc.sync.dma_start(out=run_out[r].flatten_outer_dims(), in_=units[i][:])

@@ -3,7 +3,6 @@ from concourse.masks import make_identity
 
 F32 = mybir.dt.float32
 BF16 = mybir.dt.bfloat16
-I32 = mybir.dt.int32
 U32 = mybir.dt.uint32
 U8 = mybir.dt.uint8
 FP8X4 = mybir.dt.float8_e4m3fn_x4
@@ -18,32 +17,25 @@ D = 512
 RUN = 512
 RUNS = 4
 H_PASSES = H // K_PASS
-BIAS_ROW = 2 * P
-DOWN_ROWS = D // BIAS_ROW
-RUN_ROWS = RUN // BIAS_ROW
-BIAS_ROWS = DOWN_ROWS + RUNS * RUN_ROWS
 RUNS_PER_BANK = 2
 NORMALISED = (0, 2)
-PLAIN = (1, 3)
-RUN_ORDER = NORMALISED + PLAIN
+RUN_ORDER = (0, 2, 1, 3)
 EPS = 1e-6
-DOWN_VECTOR_COLS = 320
-POST_VECTOR_COLS = 256
+HALF = D // 2
+POST_WORDS = RUNS * RUN // 2 // P
+DOWN_WORDS = D // 2 // P
+BANK_WORDS = POST_WORDS // RUNS_PER_BANK
+DOWN_PIECES = ((0, 0, 256, 208), (0, 256, 512, 256), (1, 0, 512, 320))
+POST_VECTOR_COLS = {0: 208, 2: 128, 1: 336, 3: 64}
 
 FLOPS = 2 * P * (H * D + D * RUNS * RUN)
 
 
-def regroup(nc, grouped, raw, vector_cols):
-    width = raw.shape[2]
-    for copy, cols in ((nc.vector.tensor_copy, slice(0, vector_cols)), (nc.scalar.copy, slice(vector_cols, width))):
-        copy(
-            out=grouped[:, cols, :].rearrange("p (c i) t -> p c t i", i=4),
-            in_=raw[:, :, cols].rearrange("p t (c i) -> p c t i", i=4),
-        )
-
-
-def quantise(nc, codes, scales, grouped):
-    nc.vector.quantize_mx(out=codes.bitcast(FP8X4), scales=scales, in_=grouped)
+def regroup_on(copy, grouped, raw):
+    copy(
+        out=grouped.rearrange("p (c i) t -> p c t i", i=4),
+        in_=raw.rearrange("p t (c i) -> p c t i", i=4),
+    )
 
 
 def tile_corticalcolumngroup_pb_s_kernel(
@@ -54,23 +46,20 @@ def tile_corticalcolumngroup_pb_s_kernel(
 
     with tc.tile_pool(name="keep", bufs=1) as keep, tc.psum_pool(name="psum", bufs=8) as psum, tc.manual_schedule():
 
-        act_sb = keep.tile([P, H], BF16)
-        nc.sync.dma_start(out=act_sb[:], in_=ffn_act.rearrange("s n g h -> (s n g) h"))
-        bias_rows = keep.tile([P, BIAS_ROW], BF16)
-        nc.vector.memset(bias_rows[:].bitcast(I32), 0)
-        nc.sync.dma_start(
-            out=bias_rows[0:DOWN_ROWS, :], in_=down_b.rearrange("o (r c) -> (o r) c", c=BIAS_ROW)
-        )
-        nc.sync.dma_start(
-            out=bias_rows[DOWN_ROWS:BIAS_ROWS, :], in_=post_b.rearrange("o (r c) -> (o r) c", c=BIAS_ROW)
-        )
-        down_rows = down_w.rearrange("o (g u p e) n -> (o g) p u (e n)", g=H_PASSES, u=2, e=2)
-        down_raw = []
-        for g in range(H_PASSES):
-            down_raw.append(keep.tile([P, PACK, D], BF16, name="down_raw%d" % g))
-            nc.sync.dma_start(out=down_raw[g][:].rearrange("p (u e) n -> p u (e n)", u=2), in_=down_rows[g])
+        down_b_sb = keep.tile([P, 2 * DOWN_WORDS], BF16)
+        nc.sync.dma_start(out=down_b_sb[:], in_=down_b.rearrange("o (p c) -> (o p) c", p=P))
+        post_b_sb = keep.tile([P, 2 * POST_WORDS], BF16)
+        nc.sync.dma_start(out=post_b_sb[:], in_=post_b.rearrange("o (p c) -> (o p) c", p=P))
         mix_sb = keep.tile([P, D], BF16)
         nc.sync.dma_start(out=mix_sb[:], in_=x_mix.rearrange("s n g d -> (s n g) d"))
+        down_rows = down_w.rearrange("o (g p t) n -> (o g) p t n", g=H_PASSES, t=PACK)
+        act_sb = keep.tile([P, H], BF16)
+        down_raw = []
+        for i, (g, first, last, mid) in enumerate(DOWN_PIECES):
+            down_raw.append(keep.tile([P, PACK, last - first], BF16, name="down_raw%d" % i))
+            nc.sync.dma_start(out=down_raw[i][:], in_=down_rows[g][:, :, first:last])
+            if i == 0:
+                nc.sync.dma_start(out=act_sb[:], in_=ffn_act.rearrange("s n g h -> (s n g) h"))
         post_rows = post_w.rearrange("o (t p) n -> (o p) t n", t=PACK)
         post_raw = {}
         for r in RUN_ORDER:
@@ -88,6 +77,9 @@ def tile_corticalcolumngroup_pb_s_kernel(
         down_grouped = [keep.tile([P, D, PACK], BF16, align_bytes=64, name="down_grouped%d" % g) for g in range(H_PASSES)]
         down_codes = keep.tile([P, H_PASSES, D], U32, align_bytes=64)
         down_scales = keep.tile([P, H_PASSES, D], U8, align_bytes=64)
+        act_grouped = keep.tile([P, H_PASSES * P * PACK], BF16, align_bytes=64)
+        act_codes = keep.tile([P, H_PASSES, P], U32, align_bytes=64)
+        act_scales = keep.tile([P, H_PASSES, P], U8, align_bytes=64)
         post_grouped = {}
         for r in RUN_ORDER:
             post_grouped[r] = keep.tile([P, RUN, PACK], BF16, align_bytes=64, name="post_grouped%d" % r)
@@ -95,31 +87,63 @@ def tile_corticalcolumngroup_pb_s_kernel(
         post_scales = keep.tile([P, RUNS, RUN], U8, align_bytes=64)
         x_codes = keep.tile([P, P], U32, align_bytes=64)
         x_scales = keep.tile([P, P], U8, align_bytes=64)
+        x_out = keep.tile([P, D], F32)
+        mix_bias = keep.tile([P, D], F32)
+        proj_ps = {}
         proj = {}
+        for r in RUN_ORDER:
+            proj[r] = keep.tile([P, RUN], F32, name="proj%d" % r)
+        sum_sq = keep.tile([P, len(NORMALISED)], F32)
+        above = keep.tile([P, len(NORMALISED)], F32)
+        inv_norm = keep.tile([P, len(NORMALISED)], F32)
 
-        def spread_bias_rows(first, rows):
-            bank = psum.tile([P, rows * P], F32, tag="bank", name="bias_ps%d" % first)
-            for i in range(rows):
+        def spread_words(bank, words, first):
+            for w in range(bank.shape[1] // P):
                 nc.tensor.transpose(
-                    bank[:, i * P : (i + 1) * P],
-                    bias_col[:, first + i : first + i + 1].to_broadcast([P, P]),
-                    ident[:],
+                    bank[:, w * P : (w + 1) * P], words[:, first + w : first + w + 1].to_broadcast([P, P]), ident[:]
                 )
-            return bank
+
+        def keep_post_bias(b, bank):
+            nc.scalar.copy(
+                out=post_bias[:].bitcast(F32).rearrange("q (p b w) -> q b p w", b=RUNS_PER_BANK, w=BANK_WORDS)[:, b],
+                in_=bank[:].rearrange("q (w p) -> q p w", p=P),
+            )
+
+        def regroup_down(i):
+            g, first, last, mid = DOWN_PIECES[i]
+            regroup_on(nc.vector.tensor_copy, down_grouped[g][:, first : first + mid, :], down_raw[i][:, :, 0:mid])
+            if first + mid < last:
+                regroup_on(nc.scalar.copy, down_grouped[g][:, first + mid : last, :], down_raw[i][:, :, mid:])
 
         def regroup_post(r):
-            regroup(nc, post_grouped[r], post_raw[r], POST_VECTOR_COLS)
+            mid = POST_VECTOR_COLS[r]
+            regroup_on(nc.vector.tensor_copy, post_grouped[r][:, 0:mid, :], post_raw[r][:, :, 0:mid])
+            regroup_on(nc.scalar.copy, post_grouped[r][:, mid:RUN, :], post_raw[r][:, :, mid:RUN])
 
-        def quantise_down(g):
-            quantise(nc, down_codes[:, g, :], down_scales[:, g, :], down_grouped[g][:].rearrange("p n t -> p (n t)"))
+        def quantise(codes, scales, grouped):
+            nc.vector.quantize_mx(out=codes.bitcast(FP8X4), scales=scales, in_=grouped.rearrange("p n t -> p (n t)"))
+
+        def quantise_down(g, cols=slice(0, D)):
+            quantise(down_codes[:, g, cols], down_scales[:, g, cols], down_grouped[g][:, cols, :])
 
         def quantise_post(r):
-            quantise(nc, post_codes[:, r, :], post_scales[:, r, :], post_grouped[r][:].rearrange("p n t -> p (n t)"))
+            quantise(post_codes[:, r, :], post_scales[:, r, :], post_grouped[r][:])
+
+        def multiply_down(bank, g, cols):
+            nc.tensor.matmul_mx(
+                out=bank[:],
+                lhsT=act_codes[:, g, :].bitcast(FP8X4),
+                lhsT_scale=act_scales[:, g, :],
+                rhs=down_codes[:, g, cols].bitcast(FP8X4),
+                rhs_scale=down_scales[:, g, cols],
+                start=(g == 0),
+                stop=(g == H_PASSES - 1),
+            )
 
         def project(r):
-            proj_ps = psum.tile([P, RUN], F32, tag="bank", name="proj_ps%d" % r)
+            proj_ps[r] = psum.tile([P, RUN], F32, tag="bank", name="proj_ps%d" % r)
             nc.tensor.matmul_mx(
-                out=proj_ps[:],
+                out=proj_ps[r][:],
                 lhsT=x_codes[:].bitcast(FP8X4),
                 lhsT_scale=x_scales[:],
                 rhs=post_codes[:, r, :].bitcast(FP8X4),
@@ -127,101 +151,105 @@ def tile_corticalcolumngroup_pb_s_kernel(
                 start=True,
                 stop=True,
             )
-            proj[r] = keep.tile([P, RUN], F32, name="proj%d" % r)
+
+        def add_bias(r, first=0, last=RUN):
             nc.vector.tensor_tensor(
-                out=proj[r][:], in0=proj_ps[:], in1=post_bias[:, r * RUN : (r + 1) * RUN], op=ALU.add
+                out=proj[r][:, first:last],
+                in0=proj_ps[r][:, first:last],
+                in1=post_bias[:, r * RUN + first : r * RUN + last],
+                op=ALU.add,
             )
 
-        def store_plain(r):
-            nc.sync.dma_start(out=run_out[r].flatten_outer_dims(), in_=proj[r][:])
+        def store_run(r, first=0, last=RUN):
+            nc.sync.dma_start(out=run_out[r].flatten_outer_dims()[:, first:last], in_=proj[r][:, first:last])
 
-        sum_sq = keep.tile([P, len(NORMALISED)], F32)
-        inv_norm = keep.tile([P, len(NORMALISED)], F32)
-
-        def sum_squares(i):
+        def invert_norm(i):
             squares = keep.tile([P, RUN], F32, name="squares%d" % i)
+            one_col = slice(i, i + 1)
             nc.scalar.activation(
-                out=squares[:], in_=proj[NORMALISED[i]][:], func=ACT.Square, accum_out=sum_sq[:, i : i + 1]
+                out=squares[:], in_=proj[NORMALISED[i]][:], func=ACT.Square, accum_out=sum_sq[:, one_col]
+            )
+            nc.scalar.activation(out=above[:, one_col], in_=sum_sq[:, one_col], func=ACT.Relu, bias=-EPS * EPS)
+            nc.scalar.activation(
+                out=inv_norm[:, one_col], in_=above[:, one_col], func=ACT.Abs_reciprocal_sqrt, bias=EPS * EPS
             )
 
-        def invert_norms():
-            above = keep.tile([P, len(NORMALISED)], F32)
-            nc.scalar.activation(out=above[:], in_=sum_sq[:], func=ACT.Relu, bias=-EPS * EPS)
-            nc.scalar.activation(out=inv_norm[:], in_=above[:], func=ACT.Abs_reciprocal_sqrt, bias=EPS * EPS)
+        def store_unit(i):
+            unit = keep.tile([P, RUN], F32, name="unit%d" % i)
+            nc.vector.tensor_scalar_mul(out=unit[:], in0=proj[NORMALISED[i]][:], scalar1=inv_norm[:, i : i + 1])
+            nc.sync.dma_start(out=run_out[NORMALISED[i]].flatten_outer_dims(), in_=unit[:])
 
+        down_bias_ps = psum.tile([P, DOWN_WORDS * P], F32, tag="bank")
+        spread_words(down_bias_ps, down_b_sb[:].bitcast(F32), 0)
+        post_bias_ps = []
+        for b in range(RUNS_PER_BANK):
+            post_bias_ps.append(psum.tile([P, BANK_WORDS * P], F32, tag="bank", name="post_bias_ps%d" % b))
+            spread_words(post_bias_ps[b], post_b_sb[:].bitcast(F32), BANK_WORDS * b)
+        nc.vector.tensor_tensor(
+            out=mix_bias[:].rearrange("q (p w e) -> q p w e", w=DOWN_WORDS, e=2),
+            in0=down_bias_ps[:].bitcast(BF16).rearrange("q (w p e) -> q p w e", w=DOWN_WORDS, e=2),
+            in1=mix_sb[:].rearrange("q (p w e) -> q p w e", w=DOWN_WORDS, e=2),
+            op=ALU.add,
+        )
+
+        regroup_down(0)
+        for b in range(RUNS_PER_BANK):
+            keep_post_bias(b, post_bias_ps[b])
         act_words = act_sb[:].bitcast(F32)
         act_ps = psum.tile([P, 2 * H_PASSES, P], F32, tag="bank")
-        for j in range(2 * H_PASSES):
-            nc.tensor.transpose(act_ps[:, j, :], act_words[:, j * P : (j + 1) * P], ident[:])
-        bias_col_ps = psum.tile([P, P], F32, tag="bank")
-        nc.tensor.transpose(bias_col_ps[:], bias_rows[:].bitcast(F32), ident[:])
-        bias_col = keep.tile([P, BIAS_ROWS], F32)
-        nc.vector.tensor_copy(out=bias_col[:], in_=bias_col_ps[:, 0:BIAS_ROWS])
-        down_bias_ps = spread_bias_rows(0, DOWN_ROWS)
-        post_bias_ps = [
-            spread_bias_rows(DOWN_ROWS + b * RUNS_PER_BANK * RUN_ROWS, RUNS_PER_BANK * RUN_ROWS)
-            for b in range(RUNS // RUNS_PER_BANK)
-        ]
-
-        act_grouped = keep.tile([P, H_PASSES * P * PACK], BF16, align_bytes=64)
+        for g in range(H_PASSES):
+            for u in range(2):
+                nc.tensor.transpose(act_ps[:, 2 * g + u, :], act_words[:, 2 * P * g + u : 2 * P * (g + 1) : 2], ident[:])
         nc.scalar.copy(
             out=act_grouped[:].bitcast(F32).rearrange("p (g r u) -> p g r u", g=H_PASSES, u=2),
             in_=act_ps[:].rearrange("p (g u) r -> p g r u", u=2),
         )
-        regroup(nc, down_grouped[0], down_raw[0], DOWN_VECTOR_COLS)
-        act_codes = keep.tile([P, H_PASSES * P], U32, align_bytes=64)
-        act_scales = keep.tile([P, H_PASSES * P], U8, align_bytes=64)
-        quantise(nc, act_codes[:], act_scales[:], act_grouped[:])
-        regroup(nc, down_grouped[1], down_raw[1], DOWN_VECTOR_COLS)
+        regroup_down(1)
         quantise_down(0)
-        quantise_down(1)
-        down_ps = psum.tile([P, D], F32, tag="bank")
-        for g in range(H_PASSES):
-            tokens = slice(g * P, (g + 1) * P)
-            nc.tensor.matmul_mx(
-                out=down_ps[:],
-                lhsT=act_codes[:, tokens].bitcast(FP8X4),
-                lhsT_scale=act_scales[:, tokens],
-                rhs=down_codes[:, g, :].bitcast(FP8X4),
-                rhs_scale=down_scales[:, g, :],
-                start=(g == 0),
-                stop=(g == H_PASSES - 1),
-            )
+        regroup_down(2)
+        nc.vector.quantize_mx(
+            out=act_codes[:].rearrange("p g r -> p (g r)").bitcast(FP8X4),
+            scales=act_scales[:].rearrange("p g r -> p (g r)"),
+            in_=act_grouped[:],
+        )
+        halves = [slice(h * HALF, (h + 1) * HALF) for h in range(2)]
+        down_ps = [psum.tile([P, HALF], F32, tag="bank", name="down_ps%d" % h) for h in range(2)]
+        for h in range(2):
+            multiply_down(down_ps[h], 0, halves[h])
+        for h in range(2):
+            quantise_down(1, halves[h])
+            multiply_down(down_ps[h], 1, halves[h])
 
-        bank_words = RUNS_PER_BANK * RUN // 2
-        for b in range(RUNS // RUNS_PER_BANK):
-            nc.scalar.copy(
-                out=post_bias[:].bitcast(F32)[:, b * bank_words : (b + 1) * bank_words], in_=post_bias_ps[b][:]
-            )
-        regroup_post(RUN_ORDER[0])
-        mix_bias = keep.tile([P, D], F32)
-        nc.vector.tensor_tensor(out=mix_bias[:], in0=down_bias_ps[:].bitcast(BF16), in1=mix_sb[:], op=ALU.add)
-        regroup_post(RUN_ORDER[1])
-        x_out = keep.tile([P, D], F32)
-        nc.vector.tensor_tensor(out=x_out[:], in0=down_ps[:], in1=mix_bias[:], op=ALU.add)
-        nc.sync.dma_start(out=out_0.rearrange("s n g d -> (s n g) d"), in_=x_out[:])
+        regroup_post(0)
+        regroup_post(2)
         x_ps = psum.tile([P, PACK, P], F32, tag="bank")
-        for t in range(PACK):
-            nc.tensor.transpose(x_ps[:, t, :], x_out[:, t * P : (t + 1) * P], ident[:])
-        quantise_post(RUN_ORDER[0])
-        regroup_post(RUN_ORDER[2])
+        for h in range(2):
+            nc.vector.tensor_tensor(
+                out=x_out[:, halves[h]], in0=down_ps[h][:], in1=mix_bias[:, halves[h]], op=ALU.add
+            )
+            for t in range(2 * h, 2 * h + 2):
+                nc.tensor.transpose(x_ps[:, t, :], x_out[:, t * P : (t + 1) * P], ident[:])
+        nc.sync.dma_start(out=out_0.rearrange("s n g d -> (s n g) d"), in_=x_out[:])
+        quantise_post(0)
         x_grouped = keep.tile([P, P, PACK], BF16, align_bytes=64)
         nc.scalar.copy(out=x_grouped[:], in_=x_ps[:].rearrange("p t r -> p r t"))
-        quantise_post(RUN_ORDER[1])
-        regroup_post(RUN_ORDER[3])
-        quantise(nc, x_codes[:], x_scales[:], x_grouped[:].rearrange("p r t -> p (r t)"))
-        quantise_post(RUN_ORDER[2])
-        quantise_post(RUN_ORDER[3])
+        regroup_post(1)
+        regroup_post(3)
+        quantise(x_codes[:], x_scales[:], x_grouped[:])
 
-        for i in range(len(NORMALISED)):
-            project(NORMALISED[i])
-            sum_squares(i)
-        invert_norms()
-        for r in PLAIN:
+        project(0)
+        for r in (2, 1):
+            quantise_post(r)
             project(r)
-            store_plain(r)
-        units = [keep.tile([P, RUN], F32, name="unit%d" % i) for i in range(len(NORMALISED))]
-        nc.vector.tensor_scalar_mul(out=units[0][:], in0=proj[NORMALISED[0]][:], scalar1=inv_norm[:, 0:1])
-        nc.scalar.activation(out=units[1][:], in_=proj[NORMALISED[1]][:], func=ACT.Copy, scale=inv_norm[:, 1:2])
-        for i, r in enumerate(NORMALISED):
-            nc.sync.dma_start(out=run_out[r].flatten_outer_dims(), in_=units[i][:])
+        for i in range(len(NORMALISED)):
+            add_bias(NORMALISED[i])
+            invert_norm(i)
+        quantise_post(3)
+        project(3)
+        add_bias(1)
+        store_run(1)
+        store_unit(0)
+        for first in (0, RUN // 2):
+            add_bias(3, first, first + RUN // 2)
+            store_run(3, first, first + RUN // 2)
+        store_unit(1)

@@ -21,6 +21,7 @@ RUNS_PER_BANK = 2
 NORMALISED = (0, 2)
 RUN_ORDER = (0, 2, 1, 3)
 EPS = 1e-6
+IDLE_PRODUCTS = 2
 HALF = D // 2
 POST_WORDS = RUNS * RUN // 2 // P
 DOWN_WORDS = D // 2 // P
@@ -102,6 +103,10 @@ def tile_corticalcolumngroup_pb_s_kernel(
                 nc.tensor.transpose(
                     bank[:, w * P : (w + 1) * P], words[:, first + w : first + w + 1].to_broadcast([P, P]), ident[:]
                 )
+
+        def keep_tensor_busy():
+            for i in range(IDLE_PRODUCTS):
+                nc.tensor.matmul(idle_ps[:], lhsT=ident[:], rhs=ident[:], start=True, stop=True)
 
         def keep_post_bias(b, bank):
             nc.scalar.copy(
@@ -197,9 +202,11 @@ def tile_corticalcolumngroup_pb_s_kernel(
             keep_post_bias(b, post_bias_ps[b])
         act_words = act_sb[:].bitcast(F32)
         act_ps = psum.tile([P, 2 * H_PASSES, P], F32, tag="bank")
+        idle_ps = psum.tile([P, P], F32, tag="bank")
         for g in range(H_PASSES):
             for u in range(2):
                 nc.tensor.transpose(act_ps[:, 2 * g + u, :], act_words[:, 2 * P * g + u : 2 * P * (g + 1) : 2], ident[:])
+        keep_tensor_busy()
         nc.scalar.copy(
             out=act_grouped[:].bitcast(F32).rearrange("p (g r u) -> p g r u", g=H_PASSES, u=2),
             in_=act_ps[:].rearrange("p (g u) r -> p g r u", u=2),
@@ -229,6 +236,7 @@ def tile_corticalcolumngroup_pb_s_kernel(
             )
             for t in range(2 * h, 2 * h + 2):
                 nc.tensor.transpose(x_ps[:, t, :], x_out[:, t * P : (t + 1) * P], ident[:])
+        keep_tensor_busy()
         nc.sync.dma_start(out=out_0.rearrange("s n g d -> (s n g) d"), in_=x_out[:])
         quantise_post(0)
         x_grouped = keep.tile([P, P, PACK], BF16, align_bytes=64)

@@ -3,6 +3,7 @@ from concourse.masks import make_identity
 
 F32 = mybir.dt.float32
 BF16 = mybir.dt.bfloat16
+I32 = mybir.dt.int32
 U32 = mybir.dt.uint32
 U8 = mybir.dt.uint8
 FP8X4 = mybir.dt.float8_e4m3fn_x4
@@ -23,11 +24,13 @@ RUN_ORDER = (0, 2, 1, 3)
 EPS = 1e-6
 IDLE_PRODUCTS = 2
 HALF = D // 2
-POST_WORDS = RUNS * RUN // 2 // P
-DOWN_WORDS = D // 2 // P
-BANK_WORDS = POST_WORDS // RUNS_PER_BANK
-DOWN_PIECES = ((0, 0, 256, 208), (0, 256, 512, 256), (1, 0, 512, 320))
-POST_VECTOR_COLS = {0: 208, 2: 128, 1: 336, 3: 64}
+BIAS_ROW = 2 * P
+DOWN_ROWS = D // BIAS_ROW
+RUN_ROWS = RUN // BIAS_ROW
+BIAS_ROWS = DOWN_ROWS + RUNS * RUN_ROWS
+BANK_ROWS = RUNS_PER_BANK * RUN_ROWS
+DOWN_VECTOR_COLS = (256, 384)
+POST_VECTOR_COLS = {0: 224, 2: 176, 1: 384, 3: 80}
 
 FLOPS = 2 * P * (H * D + D * RUNS * RUN)
 
@@ -45,22 +48,25 @@ def tile_corticalcolumngroup_pb_s_kernel(
     nc = tc.nc
     run_out = (out_1, out_2, out_3, out_4)
 
-    with tc.tile_pool(name="keep", bufs=1) as keep, tc.psum_pool(name="psum", bufs=8) as psum, tc.manual_schedule():
+    with tc.tile_pool(name="keep", bufs=1) as keep, tc.psum_pool(name="psum", bufs=7) as psum, tc.manual_schedule():
 
-        down_b_sb = keep.tile([P, 2 * DOWN_WORDS], BF16)
-        nc.sync.dma_start(out=down_b_sb[:], in_=down_b.rearrange("o (p c) -> (o p) c", p=P))
-        post_b_sb = keep.tile([P, 2 * POST_WORDS], BF16)
-        nc.sync.dma_start(out=post_b_sb[:], in_=post_b.rearrange("o (p c) -> (o p) c", p=P))
+        act_sb = keep.tile([P, H], BF16)
+        nc.sync.dma_start(out=act_sb[:], in_=ffn_act.rearrange("s n g h -> (s n g) h"))
+        bias_rows = keep.tile([P, BIAS_ROW], BF16)
+        nc.vector.memset(bias_rows[:].bitcast(I32), 0)
+        nc.sync.dma_start(
+            out=bias_rows[0:DOWN_ROWS, :], in_=down_b.rearrange("o (r c) -> (o r) c", c=BIAS_ROW)
+        )
+        nc.sync.dma_start(
+            out=bias_rows[DOWN_ROWS:BIAS_ROWS, :], in_=post_b.rearrange("o (r c) -> (o r) c", c=BIAS_ROW)
+        )
         mix_sb = keep.tile([P, D], BF16)
         nc.sync.dma_start(out=mix_sb[:], in_=x_mix.rearrange("s n g d -> (s n g) d"))
         down_rows = down_w.rearrange("o (g p t) n -> (o g) p t n", g=H_PASSES, t=PACK)
-        act_sb = keep.tile([P, H], BF16)
         down_raw = []
-        for i, (g, first, last, mid) in enumerate(DOWN_PIECES):
-            down_raw.append(keep.tile([P, PACK, last - first], BF16, name="down_raw%d" % i))
-            nc.sync.dma_start(out=down_raw[i][:], in_=down_rows[g][:, :, first:last])
-            if i == 0:
-                nc.sync.dma_start(out=act_sb[:], in_=ffn_act.rearrange("s n g h -> (s n g) h"))
+        for g in range(H_PASSES):
+            down_raw.append(keep.tile([P, PACK, D], BF16, name="down_raw%d" % g))
+            nc.sync.dma_start(out=down_raw[g][:], in_=down_rows[g])
         post_rows = post_w.rearrange("o (t p) n -> (o p) t n", t=PACK)
         post_raw = {}
         for r in RUN_ORDER:
@@ -98,31 +104,35 @@ def tile_corticalcolumngroup_pb_s_kernel(
         above = keep.tile([P, len(NORMALISED)], F32)
         inv_norm = keep.tile([P, len(NORMALISED)], F32)
 
-        def spread_words(bank, words, first):
-            for w in range(bank.shape[1] // P):
-                nc.tensor.transpose(
-                    bank[:, w * P : (w + 1) * P], words[:, first + w : first + w + 1].to_broadcast([P, P]), ident[:]
-                )
-
         def keep_tensor_busy():
             for i in range(IDLE_PRODUCTS):
                 nc.tensor.matmul(idle_ps[:], lhsT=ident[:], rhs=ident[:], start=True, stop=True)
 
+        def spread_bias_rows(first, rows):
+            bank = psum.tile([P, rows * P], F32, tag="bank", name="bias_ps%d" % first)
+            for i in range(rows):
+                nc.tensor.transpose(
+                    bank[:, i * P : (i + 1) * P],
+                    bias_col[:, first + i : first + i + 1].to_broadcast([P, P]),
+                    ident[:],
+                )
+            return bank
+
         def keep_post_bias(b, bank):
-            nc.scalar.copy(
-                out=post_bias[:].bitcast(F32).rearrange("q (p b w) -> q b p w", b=RUNS_PER_BANK, w=BANK_WORDS)[:, b],
-                in_=bank[:].rearrange("q (w p) -> q p w", p=P),
-            )
+            words = RUNS_PER_BANK * RUN // 2
+            nc.scalar.copy(out=post_bias[:].bitcast(F32)[:, b * words : (b + 1) * words], in_=bank[:])
 
-        def regroup_down(i):
-            g, first, last, mid = DOWN_PIECES[i]
-            regroup_on(nc.vector.tensor_copy, down_grouped[g][:, first : first + mid, :], down_raw[i][:, :, 0:mid])
-            if first + mid < last:
-                regroup_on(nc.scalar.copy, down_grouped[g][:, first + mid : last, :], down_raw[i][:, :, mid:])
+        def regroup_down(g):
+            mid = DOWN_VECTOR_COLS[g]
+            regroup_on(nc.vector.tensor_copy, down_grouped[g][:, 0:mid, :], down_raw[g][:, :, 0:mid])
+            regroup_on(nc.scalar.copy, down_grouped[g][:, mid:D, :], down_raw[g][:, :, mid:D])
 
-        def regroup_post(r):
+        def regroup_post_on_vector(r):
             mid = POST_VECTOR_COLS[r]
             regroup_on(nc.vector.tensor_copy, post_grouped[r][:, 0:mid, :], post_raw[r][:, :, 0:mid])
+
+        def regroup_post_on_scalar(r):
+            mid = POST_VECTOR_COLS[r]
             regroup_on(nc.scalar.copy, post_grouped[r][:, mid:RUN, :], post_raw[r][:, :, mid:RUN])
 
         def quantise(codes, scales, grouped):
@@ -168,12 +178,14 @@ def tile_corticalcolumngroup_pb_s_kernel(
         def store_run(r, first=0, last=RUN):
             nc.sync.dma_start(out=run_out[r].flatten_outer_dims()[:, first:last], in_=proj[r][:, first:last])
 
-        def invert_norm(i):
+        def sum_squares(i):
             squares = keep.tile([P, RUN], F32, name="squares%d" % i)
-            one_col = slice(i, i + 1)
             nc.scalar.activation(
-                out=squares[:], in_=proj[NORMALISED[i]][:], func=ACT.Square, accum_out=sum_sq[:, one_col]
+                out=squares[:], in_=proj[NORMALISED[i]][:], func=ACT.Square, accum_out=sum_sq[:, i : i + 1]
             )
+
+        def invert_norm(i):
+            one_col = slice(i, i + 1)
             nc.scalar.activation(out=above[:, one_col], in_=sum_sq[:, one_col], func=ACT.Relu, bias=-EPS * EPS)
             nc.scalar.activation(
                 out=inv_norm[:, one_col], in_=above[:, one_col], func=ACT.Abs_reciprocal_sqrt, bias=EPS * EPS
@@ -184,51 +196,45 @@ def tile_corticalcolumngroup_pb_s_kernel(
             nc.vector.tensor_scalar_mul(out=unit[:], in0=proj[NORMALISED[i]][:], scalar1=inv_norm[:, i : i + 1])
             nc.sync.dma_start(out=run_out[NORMALISED[i]].flatten_outer_dims(), in_=unit[:])
 
-        down_bias_ps = psum.tile([P, DOWN_WORDS * P], F32, tag="bank")
-        spread_words(down_bias_ps, down_b_sb[:].bitcast(F32), 0)
-        post_bias_ps = []
-        for b in range(RUNS_PER_BANK):
-            post_bias_ps.append(psum.tile([P, BANK_WORDS * P], F32, tag="bank", name="post_bias_ps%d" % b))
-            spread_words(post_bias_ps[b], post_b_sb[:].bitcast(F32), BANK_WORDS * b)
-        nc.vector.tensor_tensor(
-            out=mix_bias[:].rearrange("q (p w e) -> q p w e", w=DOWN_WORDS, e=2),
-            in0=down_bias_ps[:].bitcast(BF16).rearrange("q (w p e) -> q p w e", w=DOWN_WORDS, e=2),
-            in1=mix_sb[:].rearrange("q (p w e) -> q p w e", w=DOWN_WORDS, e=2),
-            op=ALU.add,
-        )
-
-        regroup_down(0)
-        for b in range(RUNS_PER_BANK):
-            keep_post_bias(b, post_bias_ps[b])
+        idle_ps = psum.tile([P, P], F32, tag="idle", bufs=1)
+        bias_col_ps = psum.tile([P, P], F32, tag="bank")
+        nc.tensor.transpose(bias_col_ps[:], bias_rows[:].bitcast(F32), ident[:])
+        bias_col = keep.tile([P, BIAS_ROWS], F32)
+        nc.scalar.copy(out=bias_col[:], in_=bias_col_ps[:, 0:BIAS_ROWS])
         act_words = act_sb[:].bitcast(F32)
         act_ps = psum.tile([P, 2 * H_PASSES, P], F32, tag="bank")
-        idle_ps = psum.tile([P, P], F32, tag="bank")
         for g in range(H_PASSES):
             for u in range(2):
                 nc.tensor.transpose(act_ps[:, 2 * g + u, :], act_words[:, 2 * P * g + u : 2 * P * (g + 1) : 2], ident[:])
+        down_bias_ps = spread_bias_rows(0, DOWN_ROWS)
+        post_bias_ps = [spread_bias_rows(DOWN_ROWS + b * BANK_ROWS, BANK_ROWS) for b in range(RUNS // RUNS_PER_BANK)]
         keep_tensor_busy()
+
         nc.scalar.copy(
             out=act_grouped[:].bitcast(F32).rearrange("p (g r u) -> p g r u", g=H_PASSES, u=2),
             in_=act_ps[:].rearrange("p (g u) r -> p g r u", u=2),
         )
-        regroup_down(1)
-        quantise_down(0)
-        regroup_down(2)
+        nc.vector.tensor_tensor(out=mix_bias[:], in0=down_bias_ps[:].bitcast(BF16), in1=mix_sb[:], op=ALU.add)
         nc.vector.quantize_mx(
             out=act_codes[:].rearrange("p g r -> p (g r)").bitcast(FP8X4),
             scales=act_scales[:].rearrange("p g r -> p (g r)"),
             in_=act_grouped[:],
         )
+        regroup_down(0)
+        for b in range(RUNS // RUNS_PER_BANK):
+            keep_post_bias(b, post_bias_ps[b])
+        regroup_down(1)
         halves = [slice(h * HALF, (h + 1) * HALF) for h in range(2)]
         down_ps = [psum.tile([P, HALF], F32, tag="bank", name="down_ps%d" % h) for h in range(2)]
+        quantise_down(0)
         for h in range(2):
             multiply_down(down_ps[h], 0, halves[h])
         for h in range(2):
             quantise_down(1, halves[h])
             multiply_down(down_ps[h], 1, halves[h])
 
-        regroup_post(0)
-        regroup_post(2)
+        regroup_post_on_vector(0)
+        regroup_post_on_scalar(0)
         x_ps = psum.tile([P, PACK, P], F32, tag="bank")
         for h in range(2):
             nc.vector.tensor_tensor(
@@ -239,25 +245,32 @@ def tile_corticalcolumngroup_pb_s_kernel(
         keep_tensor_busy()
         nc.sync.dma_start(out=out_0.rearrange("s n g d -> (s n g) d"), in_=x_out[:])
         quantise_post(0)
+        regroup_post_on_vector(2)
+        regroup_post_on_scalar(2)
         x_grouped = keep.tile([P, P, PACK], BF16, align_bytes=64)
         nc.scalar.copy(out=x_grouped[:], in_=x_ps[:].rearrange("p t r -> p r t"))
-        regroup_post(1)
-        regroup_post(3)
+        regroup_post_on_vector(1)
+        regroup_post_on_scalar(1)
+        regroup_post_on_scalar(3)
         quantise(x_codes[:], x_scales[:], x_grouped[:])
 
         project(0)
         for r in (2, 1):
             quantise_post(r)
             project(r)
+        keep_tensor_busy()
         for i in range(len(NORMALISED)):
             add_bias(NORMALISED[i])
+            sum_squares(i)
+        for i in range(len(NORMALISED)):
             invert_norm(i)
-        quantise_post(3)
-        project(3)
+        regroup_post_on_vector(3)
         add_bias(1)
         store_run(1)
-        store_unit(0)
+        quantise_post(3)
+        project(3)
+        for i in range(len(NORMALISED)):
+            store_unit(i)
         for first in (0, RUN // 2):
             add_bias(3, first, first + RUN // 2)
             store_run(3, first, first + RUN // 2)
-        store_unit(1)

@@ -3,7 +3,6 @@ from concourse.masks import make_identity
 
 F32 = mybir.dt.float32
 BF16 = mybir.dt.bfloat16
-I32 = mybir.dt.int32
 U32 = mybir.dt.uint32
 U8 = mybir.dt.uint8
 FP8X4 = mybir.dt.float8_e4m3fn_x4
@@ -24,13 +23,11 @@ RUN_ORDER = (0, 2, 1, 3)
 EPS = 1e-6
 IDLE_PRODUCTS = 2
 HALF = D // 2
-BIAS_ROW = 2 * P
-DOWN_ROWS = D // BIAS_ROW
-RUN_ROWS = RUN // BIAS_ROW
-BIAS_ROWS = DOWN_ROWS + RUNS * RUN_ROWS
-BANK_ROWS = RUNS_PER_BANK * RUN_ROWS
-DOWN_VECTOR_COLS = (256, 384)
-POST_VECTOR_COLS = {0: 224, 2: 176, 1: 384, 3: 80}
+POST_WORDS = RUNS * RUN // 2 // P
+DOWN_WORDS = D // 2 // P
+BANK_WORDS = POST_WORDS // RUNS_PER_BANK
+DOWN_VECTOR_COLS = (352, 320)
+POST_VECTOR_COLS = {0: 240, 2: 240, 1: 320, 3: 112}
 
 FLOPS = 2 * P * (H * D + D * RUNS * RUN)
 
@@ -50,23 +47,18 @@ def tile_corticalcolumngroup_pb_s_kernel(
 
     with tc.tile_pool(name="keep", bufs=1) as keep, tc.psum_pool(name="psum", bufs=7) as psum, tc.manual_schedule():
 
-        act_sb = keep.tile([P, H], BF16)
-        nc.sync.dma_start(out=act_sb[:], in_=ffn_act.rearrange("s n g h -> (s n g) h"))
-        bias_rows = keep.tile([P, BIAS_ROW], BF16)
-        nc.vector.memset(bias_rows[:].bitcast(I32), 0)
-        nc.sync.dma_start(
-            out=bias_rows[0:DOWN_ROWS, :], in_=down_b.rearrange("o (r c) -> (o r) c", c=BIAS_ROW)
-        )
-        nc.sync.dma_start(
-            out=bias_rows[DOWN_ROWS:BIAS_ROWS, :], in_=post_b.rearrange("o (r c) -> (o r) c", c=BIAS_ROW)
-        )
+        down_b_sb = keep.tile([P, 2 * DOWN_WORDS], BF16)
+        nc.sync.dma_start(out=down_b_sb[:], in_=down_b.rearrange("o (p c) -> (o p) c", p=P))
+        post_b_sb = keep.tile([P, 2 * POST_WORDS], BF16)
+        nc.sync.dma_start(out=post_b_sb[:], in_=post_b.rearrange("o (p c) -> (o p) c", p=P))
+        down_rows = down_w.rearrange("o (g p t) n -> (o g) p t n", g=H_PASSES, t=PACK)
+        down_raw = [keep.tile([P, PACK, D], BF16, name="down_raw%d" % g) for g in range(H_PASSES)]
+        nc.sync.dma_start(out=down_raw[0][:], in_=down_rows[0])
         mix_sb = keep.tile([P, D], BF16)
         nc.sync.dma_start(out=mix_sb[:], in_=x_mix.rearrange("s n g d -> (s n g) d"))
-        down_rows = down_w.rearrange("o (g p t) n -> (o g) p t n", g=H_PASSES, t=PACK)
-        down_raw = []
-        for g in range(H_PASSES):
-            down_raw.append(keep.tile([P, PACK, D], BF16, name="down_raw%d" % g))
-            nc.sync.dma_start(out=down_raw[g][:], in_=down_rows[g])
+        act_sb = keep.tile([P, H], BF16)
+        nc.sync.dma_start(out=act_sb[:], in_=ffn_act.rearrange("s n g h -> (s n g) h"))
+        nc.sync.dma_start(out=down_raw[1][:], in_=down_rows[1])
         post_rows = post_w.rearrange("o (t p) n -> (o p) t n", t=PACK)
         post_raw = {}
         for r in RUN_ORDER:
@@ -108,19 +100,17 @@ def tile_corticalcolumngroup_pb_s_kernel(
             for i in range(IDLE_PRODUCTS):
                 nc.tensor.matmul(idle_ps[:], lhsT=ident[:], rhs=ident[:], start=True, stop=True)
 
-        def spread_bias_rows(first, rows):
-            bank = psum.tile([P, rows * P], F32, tag="bank", name="bias_ps%d" % first)
-            for i in range(rows):
+        def spread_words(bank, words, first):
+            for w in range(bank.shape[1] // P):
                 nc.tensor.transpose(
-                    bank[:, i * P : (i + 1) * P],
-                    bias_col[:, first + i : first + i + 1].to_broadcast([P, P]),
-                    ident[:],
+                    bank[:, w * P : (w + 1) * P], words[:, first + w : first + w + 1].to_broadcast([P, P]), ident[:]
                 )
-            return bank
 
         def keep_post_bias(b, bank):
-            words = RUNS_PER_BANK * RUN // 2
-            nc.scalar.copy(out=post_bias[:].bitcast(F32)[:, b * words : (b + 1) * words], in_=bank[:])
+            nc.scalar.copy(
+                out=post_bias[:].bitcast(F32).rearrange("q (p b w) -> q b p w", b=RUNS_PER_BANK, w=BANK_WORDS)[:, b],
+                in_=bank[:].rearrange("q (w p) -> q p w", p=P),
+            )
 
         def regroup_down(g):
             mid = DOWN_VECTOR_COLS[g]
@@ -197,36 +187,42 @@ def tile_corticalcolumngroup_pb_s_kernel(
             nc.sync.dma_start(out=run_out[NORMALISED[i]].flatten_outer_dims(), in_=unit[:])
 
         idle_ps = psum.tile([P, P], F32, tag="idle", bufs=1)
-        bias_col_ps = psum.tile([P, P], F32, tag="bank")
-        nc.tensor.transpose(bias_col_ps[:], bias_rows[:].bitcast(F32), ident[:])
-        bias_col = keep.tile([P, BIAS_ROWS], F32)
-        nc.scalar.copy(out=bias_col[:], in_=bias_col_ps[:, 0:BIAS_ROWS])
+        post_bias_ps = []
+        for b in range(RUNS_PER_BANK):
+            post_bias_ps.append(psum.tile([P, BANK_WORDS * P], F32, tag="bank", name="post_bias_ps%d" % b))
+        down_bias_ps = psum.tile([P, DOWN_WORDS * P], F32, tag="bank")
+        spread_words(post_bias_ps[0], post_b_sb[:].bitcast(F32), 0)
+        spread_words(down_bias_ps, down_b_sb[:].bitcast(F32), 0)
+        spread_words(post_bias_ps[1], post_b_sb[:].bitcast(F32), BANK_WORDS)
         act_words = act_sb[:].bitcast(F32)
         act_ps = psum.tile([P, 2 * H_PASSES, P], F32, tag="bank")
         for g in range(H_PASSES):
             for u in range(2):
                 nc.tensor.transpose(act_ps[:, 2 * g + u, :], act_words[:, 2 * P * g + u : 2 * P * (g + 1) : 2], ident[:])
-        down_bias_ps = spread_bias_rows(0, DOWN_ROWS)
-        post_bias_ps = [spread_bias_rows(DOWN_ROWS + b * BANK_ROWS, BANK_ROWS) for b in range(RUNS // RUNS_PER_BANK)]
         keep_tensor_busy()
 
+        keep_post_bias(0, post_bias_ps[0])
+        regroup_down(0)
+        nc.vector.tensor_tensor(
+            out=mix_bias[:].rearrange("q (p w e) -> q p w e", w=DOWN_WORDS, e=2),
+            in0=down_bias_ps[:].bitcast(BF16).rearrange("q (w p e) -> q p w e", w=DOWN_WORDS, e=2),
+            in1=mix_sb[:].rearrange("q (p w e) -> q p w e", w=DOWN_WORDS, e=2),
+            op=ALU.add,
+        )
+        keep_post_bias(1, post_bias_ps[1])
+        quantise_down(0)
         nc.scalar.copy(
             out=act_grouped[:].bitcast(F32).rearrange("p (g r u) -> p g r u", g=H_PASSES, u=2),
             in_=act_ps[:].rearrange("p (g u) r -> p g r u", u=2),
         )
-        nc.vector.tensor_tensor(out=mix_bias[:], in0=down_bias_ps[:].bitcast(BF16), in1=mix_sb[:], op=ALU.add)
+        regroup_down(1)
         nc.vector.quantize_mx(
             out=act_codes[:].rearrange("p g r -> p (g r)").bitcast(FP8X4),
             scales=act_scales[:].rearrange("p g r -> p (g r)"),
             in_=act_grouped[:],
         )
-        regroup_down(0)
-        for b in range(RUNS // RUNS_PER_BANK):
-            keep_post_bias(b, post_bias_ps[b])
-        regroup_down(1)
         halves = [slice(h * HALF, (h + 1) * HALF) for h in range(2)]
         down_ps = [psum.tile([P, HALF], F32, tag="bank", name="down_ps%d" % h) for h in range(2)]
-        quantise_down(0)
         for h in range(2):
             multiply_down(down_ps[h], 0, halves[h])
         for h in range(2):
@@ -244,8 +240,8 @@ def tile_corticalcolumngroup_pb_s_kernel(
                 nc.tensor.transpose(x_ps[:, t, :], x_out[:, t * P : (t + 1) * P], ident[:])
         keep_tensor_busy()
         nc.sync.dma_start(out=out_0.rearrange("s n g d -> (s n g) d"), in_=x_out[:])
-        quantise_post(0)
         regroup_post_on_vector(2)
+        quantise_post(0)
         regroup_post_on_scalar(2)
         x_grouped = keep.tile([P, P, PACK], BF16, align_bytes=64)
         nc.scalar.copy(out=x_grouped[:], in_=x_ps[:].rearrange("p t r -> p r t"))

@@ -88,7 +88,6 @@ def tile_corticalcolumngroup_pb_s_kernel(
         x_scales = keep.tile([P, P], U8, align_bytes=64)
         x_out = keep.tile([P, D], F32)
         mix_bias = keep.tile([P, D], F32)
-        proj_ps = {}
         proj = {}
         for r in RUN_ORDER:
             proj[r] = keep.tile([P, RUN], F32, name="proj%d" % r)
@@ -131,8 +130,8 @@ def tile_corticalcolumngroup_pb_s_kernel(
         def quantise_down(g, cols=slice(0, D)):
             quantise(down_codes[:, g, cols], down_scales[:, g, cols], down_grouped[g][:, cols, :])
 
-        def quantise_post(r):
-            quantise(post_codes[:, r, :], post_scales[:, r, :], post_grouped[r][:])
+        def quantise_post(r, cols=slice(0, RUN)):
+            quantise(post_codes[:, r, cols], post_scales[:, r, cols], post_grouped[r][:, cols, :])
 
         def multiply_down(bank, g, cols):
             nc.tensor.matmul_mx(
@@ -145,24 +144,23 @@ def tile_corticalcolumngroup_pb_s_kernel(
                 stop=(g == H_PASSES - 1),
             )
 
-        def project(r):
-            proj_ps[r] = psum.tile([P, RUN], F32, tag="bank", name="proj_ps%d" % r)
+        def project(r, cols=slice(0, RUN)):
+            bank = psum.tile([P, cols.stop - cols.start], F32, tag="bank", name="proj_ps%d_%d" % (r, cols.start))
             nc.tensor.matmul_mx(
-                out=proj_ps[r][:],
+                out=bank[:],
                 lhsT=x_codes[:].bitcast(FP8X4),
                 lhsT_scale=x_scales[:],
-                rhs=post_codes[:, r, :].bitcast(FP8X4),
-                rhs_scale=post_scales[:, r, :],
+                rhs=post_codes[:, r, cols].bitcast(FP8X4),
+                rhs_scale=post_scales[:, r, cols],
                 start=True,
                 stop=True,
             )
+            return bank
 
-        def add_bias(r, first=0, last=RUN):
+        def add_bias(r, bank, first=0):
+            last = first + bank.shape[1]
             nc.vector.tensor_tensor(
-                out=proj[r][:, first:last],
-                in0=proj_ps[r][:, first:last],
-                in1=post_bias[:, r * RUN + first : r * RUN + last],
-                op=ALU.add,
+                out=proj[r][:, first:last], in0=bank[:], in1=post_bias[:, r * RUN + first : r * RUN + last], op=ALU.add
             )
 
         def store_run(r, first=0, last=RUN):
@@ -175,11 +173,9 @@ def tile_corticalcolumngroup_pb_s_kernel(
             )
 
         def invert_norm(i):
-            one_col = slice(i, i + 1)
-            nc.scalar.activation(out=above[:, one_col], in_=sum_sq[:, one_col], func=ACT.Relu, bias=-EPS * EPS)
-            nc.scalar.activation(
-                out=inv_norm[:, one_col], in_=above[:, one_col], func=ACT.Abs_reciprocal_sqrt, bias=EPS * EPS
-            )
+            col = slice(i, i + 1)
+            nc.scalar.activation(out=above[:, col], in_=sum_sq[:, col], func=ACT.Relu, bias=-EPS * EPS)
+            nc.scalar.activation(out=inv_norm[:, col], in_=above[:, col], func=ACT.Abs_reciprocal_sqrt, bias=EPS * EPS)
 
         def store_unit(i):
             unit = keep.tile([P, RUN], F32, name="unit%d" % i)
@@ -250,23 +246,26 @@ def tile_corticalcolumngroup_pb_s_kernel(
         regroup_post_on_scalar(3)
         quantise(x_codes[:], x_scales[:], x_grouped[:])
 
-        project(0)
+        proj_ps = {0: project(0)}
         for r in (2, 1):
             quantise_post(r)
-            project(r)
+            proj_ps[r] = project(r)
         keep_tensor_busy()
-        for i in range(len(NORMALISED)):
-            add_bias(NORMALISED[i])
+        for i, r in enumerate(NORMALISED):
+            add_bias(r, proj_ps[r])
             sum_squares(i)
-        for i in range(len(NORMALISED)):
             invert_norm(i)
         regroup_post_on_vector(3)
-        add_bias(1)
+        add_bias(1, proj_ps[1])
         store_run(1)
-        quantise_post(3)
-        project(3)
-        for i in range(len(NORMALISED)):
-            store_unit(i)
-        for first in (0, RUN // 2):
-            add_bias(3, first, first + RUN // 2)
-            store_run(3, first, first + RUN // 2)
+        last_ps = []
+        for i, half in enumerate(halves):
+            quantise_post(3, half)
+            last_ps.append(project(3, half))
+            if i == 0:
+                store_unit(0)
+        for i, half in enumerate(halves):
+            add_bias(3, last_ps[i], half.start)
+            store_run(3, half.start, half.stop)
+            if i == 0:
+                store_unit(1)

@@ -21,7 +21,7 @@ RUNS_PER_BANK = 2
 NORMALISED = (0, 2)
 RUN_ORDER = (0, 2, 1, 3)
 EPS = 1e-6
-IDLE_PRODUCTS = 2
+IDLE_PRODUCTS = 3
 HALF = D // 2
 POST_WORDS = RUNS * RUN // 2 // P
 DOWN_WORDS = D // 2 // P

import concourse.mybir as mybir
from concourse.masks import make_identity

F32 = mybir.dt.float32
BF16 = mybir.dt.bfloat16
U32 = mybir.dt.uint32
U8 = mybir.dt.uint8
FP8X4 = mybir.dt.float8_e4m3fn_x4
ACT = mybir.ActivationFunctionType
ALU = mybir.AluOpType

P = 128
PACK = 4
K_PASS = P * PACK
H = 1024
D = 512
RUN = 512
RUNS = 4
H_PASSES = H // K_PASS
RUNS_PER_BANK = 2
NORMALISED = (0, 2)
RUN_ORDER = (0, 2, 1, 3)
EPS = 1e-6
IDLE_PRODUCTS = 3
HALF = D // 2
POST_WORDS = RUNS * RUN // 2 // P
DOWN_WORDS = D // 2 // P
BANK_WORDS = POST_WORDS // RUNS_PER_BANK
DOWN_VECTOR_COLS = (352, 320)
POST_VECTOR_COLS = {0: 240, 2: 240, 1: 320, 3: 112}

FLOPS = 2 * P * (H * D + D * RUNS * RUN)


def regroup_on(copy, grouped, raw):
    copy(
        out=grouped.rearrange("p (c i) t -> p c t i", i=4),
        in_=raw.rearrange("p t (c i) -> p c t i", i=4),
    )


def tile_corticalcolumngroup_pb_s_kernel(
    tc, ffn_act, x_mix, down_w, down_b, post_w, post_b, out_0, out_1, out_2, out_3, out_4
):
    nc = tc.nc
    run_out = (out_1, out_2, out_3, out_4)

    with tc.tile_pool(name="keep", bufs=1) as keep, tc.psum_pool(name="psum", bufs=7) as psum, tc.manual_schedule():

        down_b_sb = keep.tile([P, 2 * DOWN_WORDS], BF16)
        nc.sync.dma_start(out=down_b_sb[:], in_=down_b.rearrange("o (p c) -> (o p) c", p=P))
        post_b_sb = keep.tile([P, 2 * POST_WORDS], BF16)
        nc.sync.dma_start(out=post_b_sb[:], in_=post_b.rearrange("o (p c) -> (o p) c", p=P))
        down_rows = down_w.rearrange("o (g p t) n -> (o g) p t n", g=H_PASSES, t=PACK)
        down_raw = [keep.tile([P, PACK, D], BF16, name="down_raw%d" % g) for g in range(H_PASSES)]
        nc.sync.dma_start(out=down_raw[0][:], in_=down_rows[0])
        mix_sb = keep.tile([P, D], BF16)
        nc.sync.dma_start(out=mix_sb[:], in_=x_mix.rearrange("s n g d -> (s n g) d"))
        act_sb = keep.tile([P, H], BF16)
        nc.sync.dma_start(out=act_sb[:], in_=ffn_act.rearrange("s n g h -> (s n g) h"))
        nc.sync.dma_start(out=down_raw[1][:], in_=down_rows[1])
        post_rows = post_w.rearrange("o (t p) n -> (o p) t n", t=PACK)
        post_raw = {}
        for r in RUN_ORDER:
            post_raw[r] = keep.tile([P, PACK, RUN], BF16, name="post_raw%d" % r)
            nc.sync.dma_start(out=post_raw[r][:], in_=post_rows[:, :, r * RUN : (r + 1) * RUN])

        ident = keep.tile([P, P], F32)
        make_identity(nc, ident[:])
        one = keep.tile([P, 1], F32)
        nc.vector.memset(one[:], 1.0)
        warm = keep.tile([P, 1], F32)
        nc.scalar.activation(out=warm[:], in_=one[:], func=ACT.Abs_reciprocal_sqrt)

        post_bias = keep.tile([P, RUNS * RUN], BF16)
        down_grouped = [keep.tile([P, D, PACK], BF16, align_bytes=64, name="down_grouped%d" % g) for g in range(H_PASSES)]
        down_codes = keep.tile([P, H_PASSES, D], U32, align_bytes=64)
        down_scales = keep.tile([P, H_PASSES, D], U8, align_bytes=64)
        act_grouped = keep.tile([P, H_PASSES * P * PACK], BF16, align_bytes=64)
        act_codes = keep.tile([P, H_PASSES, P], U32, align_bytes=64)
        act_scales = keep.tile([P, H_PASSES, P], U8, align_bytes=64)
        post_grouped = {}
        for r in RUN_ORDER:
            post_grouped[r] = keep.tile([P, RUN, PACK], BF16, align_bytes=64, name="post_grouped%d" % r)
        post_codes = keep.tile([P, RUNS, RUN], U32, align_bytes=64)
        post_scales = keep.tile([P, RUNS, RUN], U8, align_bytes=64)
        x_codes = keep.tile([P, P], U32, align_bytes=64)
        x_scales = keep.tile([P, P], U8, align_bytes=64)
        x_out = keep.tile([P, D], F32)
        mix_bias = keep.tile([P, D], F32)
        proj = {}
        for r in RUN_ORDER:
            proj[r] = keep.tile([P, RUN], F32, name="proj%d" % r)
        sum_sq = keep.tile([P, len(NORMALISED)], F32)
        above = keep.tile([P, len(NORMALISED)], F32)
        inv_norm = keep.tile([P, len(NORMALISED)], F32)

        def keep_tensor_busy():
            for i in range(IDLE_PRODUCTS):
                nc.tensor.matmul(idle_ps[:], lhsT=ident[:], rhs=ident[:], start=True, stop=True)

        def spread_words(bank, words, first):
            for w in range(bank.shape[1] // P):
                nc.tensor.transpose(
                    bank[:, w * P : (w + 1) * P], words[:, first + w : first + w + 1].to_broadcast([P, P]), ident[:]
                )

        def keep_post_bias(b, bank):
            nc.scalar.copy(
                out=post_bias[:].bitcast(F32).rearrange("q (p b w) -> q b p w", b=RUNS_PER_BANK, w=BANK_WORDS)[:, b],
                in_=bank[:].rearrange("q (w p) -> q p w", p=P),
            )

        def regroup_down(g):
            mid = DOWN_VECTOR_COLS[g]
            regroup_on(nc.vector.tensor_copy, down_grouped[g][:, 0:mid, :], down_raw[g][:, :, 0:mid])
            regroup_on(nc.scalar.copy, down_grouped[g][:, mid:D, :], down_raw[g][:, :, mid:D])

        def regroup_post_on_vector(r):
            mid = POST_VECTOR_COLS[r]
            regroup_on(nc.vector.tensor_copy, post_grouped[r][:, 0:mid, :], post_raw[r][:, :, 0:mid])

        def regroup_post_on_scalar(r):
            mid = POST_VECTOR_COLS[r]
            regroup_on(nc.scalar.copy, post_grouped[r][:, mid:RUN, :], post_raw[r][:, :, mid:RUN])

        def quantise(codes, scales, grouped):
            nc.vector.quantize_mx(out=codes.bitcast(FP8X4), scales=scales, in_=grouped.rearrange("p n t -> p (n t)"))

        def quantise_down(g, cols=slice(0, D)):
            quantise(down_codes[:, g, cols], down_scales[:, g, cols], down_grouped[g][:, cols, :])

        def quantise_post(r, cols=slice(0, RUN)):
            quantise(post_codes[:, r, cols], post_scales[:, r, cols], post_grouped[r][:, cols, :])

        def multiply_down(bank, g, cols):
            nc.tensor.matmul_mx(
                out=bank[:],
                lhsT=act_codes[:, g, :].bitcast(FP8X4),
                lhsT_scale=act_scales[:, g, :],
                rhs=down_codes[:, g, cols].bitcast(FP8X4),
                rhs_scale=down_scales[:, g, cols],
                start=(g == 0),
                stop=(g == H_PASSES - 1),
            )

        def project(r, cols=slice(0, RUN)):
            bank = psum.tile([P, cols.stop - cols.start], F32, tag="bank", name="proj_ps%d_%d" % (r, cols.start))
            nc.tensor.matmul_mx(
                out=bank[:],
                lhsT=x_codes[:].bitcast(FP8X4),
                lhsT_scale=x_scales[:],
                rhs=post_codes[:, r, cols].bitcast(FP8X4),
                rhs_scale=post_scales[:, r, cols],
                start=True,
                stop=True,
            )
            return bank

        def add_bias(r, bank, first=0):
            last = first + bank.shape[1]
            nc.vector.tensor_tensor(
                out=proj[r][:, first:last], in0=bank[:], in1=post_bias[:, r * RUN + first : r * RUN + last], op=ALU.add
            )

        def store_run(r, first=0, last=RUN):
            nc.sync.dma_start(out=run_out[r].flatten_outer_dims()[:, first:last], in_=proj[r][:, first:last])

        def sum_squares(i):
            squares = keep.tile([P, RUN], F32, name="squares%d" % i)
            nc.scalar.activation(
                out=squares[:], in_=proj[NORMALISED[i]][:], func=ACT.Square, accum_out=sum_sq[:, i : i + 1]
            )

        def invert_norm(i):
            col = slice(i, i + 1)
            nc.scalar.activation(out=above[:, col], in_=sum_sq[:, col], func=ACT.Relu, bias=-EPS * EPS)
            nc.scalar.activation(out=inv_norm[:, col], in_=above[:, col], func=ACT.Abs_reciprocal_sqrt, bias=EPS * EPS)

        def store_unit(i):
            unit = keep.tile([P, RUN], F32, name="unit%d" % i)
            nc.vector.tensor_scalar_mul(out=unit[:], in0=proj[NORMALISED[i]][:], scalar1=inv_norm[:, i : i + 1])
            nc.sync.dma_start(out=run_out[NORMALISED[i]].flatten_outer_dims(), in_=unit[:])

        idle_ps = psum.tile([P, P], F32, tag="idle", bufs=1)
        post_bias_ps = []
        for b in range(RUNS_PER_BANK):
            post_bias_ps.append(psum.tile([P, BANK_WORDS * P], F32, tag="bank", name="post_bias_ps%d" % b))
        down_bias_ps = psum.tile([P, DOWN_WORDS * P], F32, tag="bank")
        spread_words(post_bias_ps[0], post_b_sb[:].bitcast(F32), 0)
        spread_words(down_bias_ps, down_b_sb[:].bitcast(F32), 0)
        spread_words(post_bias_ps[1], post_b_sb[:].bitcast(F32), BANK_WORDS)
        act_words = act_sb[:].bitcast(F32)
        act_ps = psum.tile([P, 2 * H_PASSES, P], F32, tag="bank")
        for g in range(H_PASSES):
            for u in range(2):
                nc.tensor.transpose(act_ps[:, 2 * g + u, :], act_words[:, 2 * P * g + u : 2 * P * (g + 1) : 2], ident[:])
        keep_tensor_busy()

        keep_post_bias(0, post_bias_ps[0])
        regroup_down(0)
        nc.vector.tensor_tensor(
            out=mix_bias[:].rearrange("q (p w e) -> q p w e", w=DOWN_WORDS, e=2),
            in0=down_bias_ps[:].bitcast(BF16).rearrange("q (w p e) -> q p w e", w=DOWN_WORDS, e=2),
            in1=mix_sb[:].rearrange("q (p w e) -> q p w e", w=DOWN_WORDS, e=2),
            op=ALU.add,
        )
        keep_post_bias(1, post_bias_ps[1])
        quantise_down(0)
        nc.scalar.copy(
            out=act_grouped[:].bitcast(F32).rearrange("p (g r u) -> p g r u", g=H_PASSES, u=2),
            in_=act_ps[:].rearrange("p (g u) r -> p g r u", u=2),
        )
        regroup_down(1)
        nc.vector.quantize_mx(
            out=act_codes[:].rearrange("p g r -> p (g r)").bitcast(FP8X4),
            scales=act_scales[:].rearrange("p g r -> p (g r)"),
            in_=act_grouped[:],
        )
        halves = [slice(h * HALF, (h + 1) * HALF) for h in range(2)]
        down_ps = [psum.tile([P, HALF], F32, tag="bank", name="down_ps%d" % h) for h in range(2)]
        for h in range(2):
            multiply_down(down_ps[h], 0, halves[h])
        for h in range(2):
            quantise_down(1, halves[h])
            multiply_down(down_ps[h], 1, halves[h])

        regroup_post_on_vector(0)
        regroup_post_on_scalar(0)
        x_ps = psum.tile([P, PACK, P], F32, tag="bank")
        for h in range(2):
            nc.vector.tensor_tensor(
                out=x_out[:, halves[h]], in0=down_ps[h][:], in1=mix_bias[:, halves[h]], op=ALU.add
            )
            for t in range(2 * h, 2 * h + 2):
                nc.tensor.transpose(x_ps[:, t, :], x_out[:, t * P : (t + 1) * P], ident[:])
        keep_tensor_busy()
        nc.sync.dma_start(out=out_0.rearrange("s n g d -> (s n g) d"), in_=x_out[:])
        regroup_post_on_vector(2)
        quantise_post(0)
        regroup_post_on_scalar(2)
        x_grouped = keep.tile([P, P, PACK], BF16, align_bytes=64)
        nc.scalar.copy(out=x_grouped[:], in_=x_ps[:].rearrange("p t r -> p r t"))
        regroup_post_on_vector(1)
        regroup_post_on_scalar(1)
        regroup_post_on_scalar(3)
        quantise(x_codes[:], x_scales[:], x_grouped[:])

        proj_ps = {0: project(0)}
        for r in (2, 1):
            quantise_post(r)
            proj_ps[r] = project(r)
        keep_tensor_busy()
        for i, r in enumerate(NORMALISED):
            add_bias(r, proj_ps[r])
            sum_squares(i)
            invert_norm(i)
        regroup_post_on_vector(3)
        add_bias(1, proj_ps[1])
        store_run(1)
        last_ps = []
        for i, half in enumerate(halves):
            quantise_post(3, half)
            last_ps.append(project(3, half))
            if i == 0:
                store_unit(0)
        for i, half in enumerate(halves):
            add_bias(3, last_ps[i], half.start)
            store_run(3, half.start, half.stop)
            if i == 0:
                store_unit(1)
